import numpy as np
import ml_dtypes


def mxq(x, axis, fmt="e4m3"):
    dtype, down = {"e4m3": (ml_dtypes.float8_e4m3fn, 7), "e5m2": (ml_dtypes.float8_e5m2, 14)}[fmt]
    v = np.moveaxis(np.asarray(x, np.float32).astype(ml_dtypes.bfloat16).astype(np.float64), axis, -1)
    blocks = v.reshape(v.shape[:-1] + (-1, 32))
    amax = np.abs(blocks).max(-1, keepdims=True)
    byte = np.maximum(np.where(amax > 0, np.frexp(amax)[1] - 1 + 127, 0) - down, 1)
    scale = np.exp2(byte - 127.0)
    codes = (blocks / scale).astype(np.float32).astype(dtype).astype(np.float64)
    return np.moveaxis((codes * scale).reshape(v.shape), -1, axis)


WIDE = False


def mx_kscale(k):
    if not WIDE:
        return np.ones(k)
    levels = np.array([20, -20, 10, -10, 0])
    a = np.random.permutation(np.resize(levels, k // 512 * 4)).reshape(k // 512, 4)
    idx = np.arange(k)
    return np.exp2(a[idx // 512, idx % 128 // 32])


BF16 = ml_dtypes.bfloat16


def bf(x):
    return np.asarray(x, np.float32).astype(BF16)


def f64(x):
    return np.asarray(x).astype(np.float64)


B, F, D, L1, L2, L3 = 32, 64, 32, 256, 256, 512
H2 = L2 // 2
K3 = H2 * F
T = B * D


def interact(h, x0):
    z = h.transpose(0, 2, 1)[:, :, :, None] * x0.transpose(0, 2, 1)[:, :, None, :]
    return z.reshape(z.shape[0], z.shape[1], -1)


def setup_inputs():
    a = mx_kscale(T).reshape(B, D)[:, 0]
    h0 = bf(np.maximum(np.random.standard_normal((B, H2, D)) * 0.75, 0.0))
    x0 = bf(np.random.standard_normal((B, F, D)))
    W3 = bf(np.random.standard_normal((K3, L3)) / np.sqrt(K3))
    b3 = bf(np.random.standard_normal(L3) * 0.2)
    g = bf(np.random.standard_normal((B, L3)) * np.exp2(np.random.randint(-12, 1, (B, 1))) / a[:, None])
    pre = interact(f64(h0), f64(x0)) @ f64(W3) + f64(b3)
    return {"h2": bf(f64(h0) * a[:, None, None]), "x0": x0, "W3": W3, "b3": b3,
            "pre": np.asarray(pre, np.float32), "grad_out": g}


def reference(h2, x0, W3, b3, pre, grad_out):
    z = interact(f64(h2), f64(x0)).reshape(T, K3)
    dp = (f64(grad_out)[:, None, :] * (f64(pre) > 0.0)).reshape(T, L3)
    return mxq(z, 0, "e4m3").T @ mxq(dp, 0, "e5m2")

@@ -1,0 +1,147 @@
+from contextlib import ExitStack
+
+import concourse.mybir as mybir
+from concourse.masks import make_identity
+
+F32 = mybir.dt.float32
+BF16 = mybir.dt.bfloat16
+U32 = mybir.dt.uint32
+U8 = mybir.dt.uint8
+E4M3X4 = mybir.dt.float8_e4m3fn_x4
+E5M2X4 = mybir.dt.float8_e5m2_x4
+ALU = mybir.AluOpType
+ACT = mybir.ActivationFunctionType
+
+P = 128
+PACK = 4
+PASSES = 2
+B, F_H, F_X, D, N = 32, 128, 64, 32, 512
+B_PASS = B // PASSES
+F_GROUP = 8
+GROUPS = F_H // F_GROUP
+COLS = F_GROUP * F_X
+M_TILES = COLS // P
+
+FLOPS = 2 * B * D * F_H * F_X * N
+BYTES = 2 * (B * F_H * D + B * F_X * D + B * N) + 4 * B * D * N + 4 * F_H * F_X * N
+
+
+def tile_cin_pb_v_kernel(tc, h2, x0, W3, b3, pre, grad_out, out):
+    nc = tc.nc
+    with ExitStack() as ctx:
+        keep = ctx.enter_context(tc.tile_pool(name="keep", bufs=1))
+        products = ctx.enter_context(tc.tile_pool(name="products", bufs=3))
+        quantised = ctx.enter_context(tc.tile_pool(name="quantised", bufs=4))
+        results = ctx.enter_context(tc.tile_pool(name="results", bufs=4))
+        psum = ctx.enter_context(tc.psum_pool(name="psum", bufs=8))
+
+        h2_rows = keep.tile([P, PASSES * B_PASS * D], BF16)
+        x0_rows = keep.tile([P, B_PASS * D], BF16)
+        grad_rows = keep.tile([P, N], BF16)
+        nc.vector.memset(grad_rows[:], 0.0)
+        nc.scalar.dma_start(out=grad_rows[0:B, :], in_=grad_out)
+        for c in range(PASSES):
+            batch = slice(c * B_PASS, (c + 1) * B_PASS)
+            nc.sync.dma_start(
+                out=x0_rows[c * F_X : (c + 1) * F_X, :].rearrange("g (b d) -> g b d", d=D),
+                in_=x0[batch].rearrange("b g d -> g b d"),
+            )
+        for c in range(PASSES):
+            batch = slice(c * B_PASS, (c + 1) * B_PASS)
+            nc.sync.dma_start(
+                out=h2_rows[:, c * B_PASS * D : (c + 1) * B_PASS * D].rearrange("f (b d) -> f b d", d=D),
+                in_=h2[batch].rearrange("b f d -> f b d"),
+            )
+        pre_rows = pre.rearrange("b d n -> (b d) n").rearrange("(c p j) n -> c p j n", c=PASSES, j=PACK)
+        pre_sb = []
+        for c in range(PASSES):
+            pre_c = keep.tile([P, PACK, N], F32, name="pre_sb%d" % c)
+            nc.sync.dma_start(out=pre_c[:], in_=pre_rows[c])
+            pre_sb.append(pre_c)
+
+        identity = keep.tile([P, P], F32)
+        make_identity(nc, identity[:])
+
+        h2_words = h2_rows[:].bitcast(F32).rearrange("f (c p u) -> f c u p", c=PASSES, u=2)
+        x0_words = x0_rows[:].bitcast(F32).rearrange("q (p u) -> q u p", u=2)
+        x0_turned = psum.tile([P, 2, P], F32, tag="bank")
+        for u in range(2):
+            nc.tensor.transpose(out=x0_turned[:, u, :], in_=x0_words[:, u, :], identity=identity[:])
+        h2_turned = psum.tile([P, PASSES, 2, P], F32, tag="bank")
+        for c in range(PASSES):
+            for u in range(2):
+                nc.tensor.transpose(out=h2_turned[:, c, u, :], in_=h2_words[:, c, u, :], identity=identity[:])
+        x0_tok = keep.tile([P, PASSES, F_X, PACK], BF16)
+        nc.scalar.copy(
+            out=x0_tok[:].bitcast(F32),
+            in_=x0_turned[:].rearrange("p u (c g) -> p c g u", c=PASSES),
+        )
+        h2_tok = keep.tile([P, GROUPS, PASSES, F_GROUP, PACK], BF16)
+        for c in range(PASSES):
+            nc.vector.tensor_copy(
+                out=h2_tok[:].bitcast(F32)[:, :, c, :, :],
+                in_=h2_turned[:, c, :, :].rearrange("p u (s f) -> p s f u", f=F_GROUP),
+            )
+
+        spread = keep.tile([P, B, P // B_PASS], BF16)
+        nc.vector.tensor_copy(
+            out=spread[:], in_=identity[:, 0:B].unsqueeze(2).to_broadcast([P, B, P // B_PASS])
+        )
+        spread_cols = spread[:].rearrange("k b r -> k (b r)")
+        dp_codes = keep.tile([P, PASSES, N], U32, align_bytes=64)
+        dp_scales = keep.tile([P, PASSES, N], U8, align_bytes=64)
+        for c in range(PASSES):
+            grad_tok = psum.tile([P, N], F32, tag="bank")
+            nc.tensor.matmul(
+                out=grad_tok[:], lhsT=spread_cols[:, c * P : (c + 1) * P], rhs=grad_rows[:], start=True, stop=True
+            )
+            sign = keep.tile([P, N, PACK], BF16, name="sign%d" % c)
+            nc.scalar.activation(out=sign[:], in_=pre_sb[c][:].rearrange("p j n -> p n j"), func=ACT.Sign)
+            dp = keep.tile([P, N, PACK], BF16, name="dp%d" % c, align_bytes=64)
+            nc.vector.scalar_tensor_tensor(
+                out=dp[:],
+                in0=sign[:],
+                scalar=0.0,
+                in1=grad_tok[:].unsqueeze(2).to_broadcast([P, N, PACK]),
+                op0=ALU.max,
+                op1=ALU.mult,
+            )
+            nc.vector.quantize_mx(
+                out=dp_codes[:, c, :].bitcast(E5M2X4),
+                scales=dp_scales[:, c, :],
+                in_=dp[:].rearrange("p n j -> p (n j)"),
+            )
+
+        out_groups = out.rearrange("(s i m) n -> s m i n", i=M_TILES, m=P)
+        shape = [P, PASSES, F_GROUP, F_X, PACK]
+        for s in range(GROUPS):
+            z = products.tile(shape, BF16, align_bytes=64)
+            nc.vector.tensor_tensor(
+                out=z[:],
+                in0=h2_tok[:, s].unsqueeze(3).to_broadcast(shape),
+                in1=x0_tok[:].unsqueeze(2).to_broadcast(shape),
+                op=ALU.mult,
+            )
+            z_codes = quantised.tile([P, PASSES, COLS], U32, align_bytes=64)
+            z_scales = quantised.tile([P, PASSES, COLS], U8, align_bytes=64)
+            nc.vector.quantize_mx(
+                out=z_codes[:].rearrange("p c w -> p (c w)").bitcast(E4M3X4),
+                scales=z_scales[:].rearrange("p c w -> p (c w)"),
+                in_=z[:].rearrange("p c f g j -> p (c f g j)"),
+            )
+            result = results.tile([P, M_TILES, N], F32)
+            for i in range(M_TILES):
+                cols = slice(i * P, (i + 1) * P)
+                acc = psum.tile([P, N], F32, tag="bank")
+                for c in range(PASSES):
+                    nc.tensor.matmul_mx(
+                        out=acc[:],
+                        lhsT=z_codes[:, c, cols].bitcast(E4M3X4),
+                        lhsT_scale=z_scales[:, c, cols],
+                        rhs=dp_codes[:, c, :].bitcast(E5M2X4),
+                        rhs_scale=dp_scales[:, c, :],
+                        start=(c == 0),
+                        stop=(c == PASSES - 1),
+                    )
+                nc.scalar.copy(out=result[:, i, :], in_=acc[:])
+            nc.sync.dma_start(out=out_groups[s], in_=result[:])

@@ -17,40 +17,48 @@ PACK = 4
 PASSES = 2
 B, F_H, F_X, D, N = 32, 128, 64, 32, 512
 B_PASS = B // PASSES
+TOKENS = B_PASS * D
+F_TILE = P // F_X
 F_GROUP = 8
-GROUPS = F_H // F_GROUP
-COLS = F_GROUP * F_X
-M_TILES = COLS // P
+AHEAD = 2
 
 FLOPS = 2 * B * D * F_H * F_X * N
 BYTES = 2 * (B * F_H * D + B * F_X * D + B * N) + 4 * B * D * N + 4 * F_H * F_X * N
+
+
+def cut_into_pieces():
+    pieces = [(first, F_GROUP) for first in range(0, F_H - F_GROUP, F_GROUP)]
+    first = F_H - F_GROUP
+    for width in (F_GROUP // 2, F_GROUP // 4, F_GROUP // 4):
+        pieces.append((first, width))
+        first += width
+    return pieces
 
 
 def tile_cin_pb_v_kernel(tc, h2, x0, W3, b3, pre, grad_out, out):
     nc = tc.nc
     with ExitStack() as ctx:
         keep = ctx.enter_context(tc.tile_pool(name="keep", bufs=1))
-        products = ctx.enter_context(tc.tile_pool(name="products", bufs=3))
+        products = ctx.enter_context(tc.tile_pool(name="products", bufs=AHEAD + 1))
         quantised = ctx.enter_context(tc.tile_pool(name="quantised", bufs=4))
         results = ctx.enter_context(tc.tile_pool(name="results", bufs=4))
         psum = ctx.enter_context(tc.psum_pool(name="psum", bufs=8))
+        ctx.enter_context(tc.manual_schedule())
 
-        h2_rows = keep.tile([P, PASSES * B_PASS * D], BF16)
-        x0_rows = keep.tile([P, B_PASS * D], BF16)
+        h2_rows = keep.tile([P, PASSES * TOKENS], BF16)
+        x0_rows = keep.tile([P, TOKENS], BF16)
         grad_rows = keep.tile([P, N], BF16)
         nc.vector.memset(grad_rows[:], 0.0)
         nc.scalar.dma_start(out=grad_rows[0:B, :], in_=grad_out)
         for c in range(PASSES):
-            batch = slice(c * B_PASS, (c + 1) * B_PASS)
             nc.sync.dma_start(
                 out=x0_rows[c * F_X : (c + 1) * F_X, :].rearrange("g (b d) -> g b d", d=D),
-                in_=x0[batch].rearrange("b g d -> g b d"),
+                in_=x0[c * B_PASS : (c + 1) * B_PASS].rearrange("b g d -> g b d"),
             )
         for c in range(PASSES):
-            batch = slice(c * B_PASS, (c + 1) * B_PASS)
             nc.sync.dma_start(
-                out=h2_rows[:, c * B_PASS * D : (c + 1) * B_PASS * D].rearrange("f (b d) -> f b d", d=D),
-                in_=h2[batch].rearrange("b f d -> f b d"),
+                out=h2_rows[:, c * TOKENS : (c + 1) * TOKENS].rearrange("f (b d) -> f b d", d=D),
+                in_=h2[c * B_PASS : (c + 1) * B_PASS].rearrange("b f d -> f b d"),
             )
         pre_rows = pre.rearrange("b d n -> (b d) n").rearrange("(c p j) n -> c p j n", c=PASSES, j=PACK)
         pre_sb = []
@@ -61,33 +69,50 @@ def tile_cin_pb_v_kernel(tc, h2, x0, W3, b3, pre, grad_out, out):
 
         identity = keep.tile([P, P], F32)
         make_identity(nc, identity[:])
-
-        h2_words = h2_rows[:].bitcast(F32).rearrange("f (c p u) -> f c u p", c=PASSES, u=2)
-        x0_words = x0_rows[:].bitcast(F32).rearrange("q (p u) -> q u p", u=2)
-        x0_turned = psum.tile([P, 2, P], F32, tag="bank")
-        for u in range(2):
-            nc.tensor.transpose(out=x0_turned[:, u, :], in_=x0_words[:, u, :], identity=identity[:])
-        h2_turned = psum.tile([P, PASSES, 2, P], F32, tag="bank")
-        for c in range(PASSES):
-            for u in range(2):
-                nc.tensor.transpose(out=h2_turned[:, c, u, :], in_=h2_words[:, c, u, :], identity=identity[:])
-        x0_tok = keep.tile([P, PASSES, F_X, PACK], BF16)
-        nc.scalar.copy(
-            out=x0_tok[:].bitcast(F32),
-            in_=x0_turned[:].rearrange("p u (c g) -> p c g u", c=PASSES),
-        )
-        h2_tok = keep.tile([P, GROUPS, PASSES, F_GROUP, PACK], BF16)
-        for c in range(PASSES):
-            nc.vector.tensor_copy(
-                out=h2_tok[:].bitcast(F32)[:, :, c, :, :],
-                in_=h2_turned[:, c, :, :].rearrange("p u (s f) -> p s f u", f=F_GROUP),
-            )
-
         spread = keep.tile([P, B, P // B_PASS], BF16)
         nc.vector.tensor_copy(
             out=spread[:], in_=identity[:, 0:B].unsqueeze(2).to_broadcast([P, B, P // B_PASS])
         )
         spread_cols = spread[:].rearrange("k b r -> k (b r)")
+
+        x0_words = x0_rows[:].bitcast(F32).rearrange("q (p u) -> q u p", u=2)
+        x0_turned = psum.tile([P, 2, P], F32, tag="bank")
+        for u in range(2):
+            nc.tensor.transpose(out=x0_turned[:, u, :], in_=x0_words[:, u, :], identity=identity[:])
+        x0_tok = keep.tile([P, PASSES, F_X, PACK], BF16)
+        nc.scalar.copy(
+            out=x0_tok[:].bitcast(F32),
+            in_=x0_turned[:].rearrange("p u (c g) -> p c g u", c=PASSES),
+        )
+        h2_words = h2_rows[:].bitcast(F32).rearrange("f (c p u) -> f c u p", c=PASSES, u=2)
+        h2_turned = psum.tile([P, PASSES, 2, P], F32, tag="bank")
+        h2_tok = keep.tile([P, PASSES, F_H, PACK], BF16)
+        for c in range(PASSES):
+            for u in range(2):
+                nc.tensor.transpose(out=h2_turned[:, c, u, :], in_=h2_words[:, c, u, :], identity=identity[:])
+            nc.vector.tensor_copy(
+                out=h2_tok[:, c].bitcast(F32), in_=h2_turned[:, c].rearrange("p u f -> p f u")
+            )
+
+        pieces = cut_into_pieces()
+        z_tiles = {}
+
+        def product(index, c):
+            first, width = pieces[index]
+            if c == 0:
+                z_tiles[index] = products.tile([P, PASSES, width, F_X, PACK], BF16, name="z", align_bytes=64)
+            shape = [P, width, F_X, PACK]
+            nc.vector.tensor_tensor(
+                out=z_tiles[index][:, c],
+                in0=h2_tok[:, c, first : first + width, :].unsqueeze(2).to_broadcast(shape),
+                in1=x0_tok[:, c].unsqueeze(1).to_broadcast(shape),
+                op=ALU.mult,
+            )
+
+        for c in range(PASSES):
+            for index in range(AHEAD):
+                product(index, c)
+
         dp_codes = keep.tile([P, PASSES, N], U32, align_bytes=64)
         dp_scales = keep.tile([P, PASSES, N], U8, align_bytes=64)
         for c in range(PASSES):
@@ -112,36 +137,33 @@ def tile_cin_pb_v_kernel(tc, h2, x0, W3, b3, pre, grad_out, out):
                 in_=dp[:].rearrange("p n j -> p (n j)"),
             )
 
-        out_groups = out.rearrange("(s i m) n -> s m i n", i=M_TILES, m=P)
-        shape = [P, PASSES, F_GROUP, F_X, PACK]
-        for s in range(GROUPS):
-            z = products.tile(shape, BF16, align_bytes=64)
-            nc.vector.tensor_tensor(
-                out=z[:],
-                in0=h2_tok[:, s].unsqueeze(3).to_broadcast(shape),
-                in1=x0_tok[:].unsqueeze(2).to_broadcast(shape),
-                op=ALU.mult,
-            )
-            z_codes = quantised.tile([P, PASSES, COLS], U32, align_bytes=64)
-            z_scales = quantised.tile([P, PASSES, COLS], U8, align_bytes=64)
+        for index in range(len(pieces)):
+            first, width = pieces[index]
+            if index + AHEAD < len(pieces):
+                for c in range(PASSES):
+                    product(index + AHEAD, c)
+            cols = width * F_X
+            z_codes = quantised.tile([P, PASSES, cols], U32, align_bytes=64)
+            z_scales = quantised.tile([P, PASSES, cols], U8, align_bytes=64)
             nc.vector.quantize_mx(
                 out=z_codes[:].rearrange("p c w -> p (c w)").bitcast(E4M3X4),
                 scales=z_scales[:].rearrange("p c w -> p (c w)"),
-                in_=z[:].rearrange("p c f g j -> p (c f g j)"),
+                in_=z_tiles[index][:].rearrange("p c f g j -> p (c f g j)"),
             )
-            result = results.tile([P, M_TILES, N], F32)
-            for i in range(M_TILES):
-                cols = slice(i * P, (i + 1) * P)
+            m_tiles = width // F_TILE
+            result = results.tile([P, m_tiles, N], F32)
+            for i in range(m_tiles):
                 acc = psum.tile([P, N], F32, tag="bank")
                 for c in range(PASSES):
                     nc.tensor.matmul_mx(
                         out=acc[:],
-                        lhsT=z_codes[:, c, cols].bitcast(E4M3X4),
-                        lhsT_scale=z_scales[:, c, cols],
+                        lhsT=z_codes[:, c, i * P : (i + 1) * P].bitcast(E4M3X4),
+                        lhsT_scale=z_scales[:, c, i * P : (i + 1) * P],
                         rhs=dp_codes[:, c, :].bitcast(E5M2X4),
                         rhs_scale=dp_scales[:, c, :],
                         start=(c == 0),
                         stop=(c == PASSES - 1),
                     )
                 nc.scalar.copy(out=result[:, i, :], in_=acc[:])
-            nc.sync.dma_start(out=out_groups[s], in_=result[:])
+            rows = out[first * F_X : (first + width) * F_X, :]
+            nc.sync.dma_start(out=rows.rearrange("(i m) n -> m i n", m=P), in_=result[:])

@@ -20,7 +20,7 @@ B_PASS = B // PASSES
 TOKENS = B_PASS * D
 F_TILE = P // F_X
 F_GROUP = 8
-AHEAD = 2
+AHEAD = 3
 
 FLOPS = 2 * B * D * F_H * F_X * N
 BYTES = 2 * (B * F_H * D + B * F_X * D + B * N) + 4 * B * D * N + 4 * F_H * F_X * N
@@ -39,7 +39,7 @@ def tile_cin_pb_v_kernel(tc, h2, x0, W3, b3, pre, grad_out, out):
     nc = tc.nc
     with ExitStack() as ctx:
         keep = ctx.enter_context(tc.tile_pool(name="keep", bufs=1))
-        products = ctx.enter_context(tc.tile_pool(name="products", bufs=AHEAD + 1))
+        products = ctx.enter_context(tc.tile_pool(name="products", bufs=AHEAD + 2))
         quantised = ctx.enter_context(tc.tile_pool(name="quantised", bufs=4))
         results = ctx.enter_context(tc.tile_pool(name="results", bufs=4))
         psum = ctx.enter_context(tc.psum_pool(name="psum", bufs=8))
@@ -86,35 +86,45 @@ def tile_cin_pb_v_kernel(tc, h2, x0, W3, b3, pre, grad_out, out):
         )
         h2_words = h2_rows[:].bitcast(F32).rearrange("f (c p u) -> f c u p", c=PASSES, u=2)
         h2_turned = psum.tile([P, PASSES, 2, P], F32, tag="bank")
-        h2_tok = keep.tile([P, PASSES, F_H, PACK], BF16)
+        h2_tok = keep.tile([P, F_H // F_GROUP, PASSES, F_GROUP, PACK], BF16)
         for c in range(PASSES):
             for u in range(2):
                 nc.tensor.transpose(out=h2_turned[:, c, u, :], in_=h2_words[:, c, u, :], identity=identity[:])
             nc.vector.tensor_copy(
-                out=h2_tok[:, c].bitcast(F32), in_=h2_turned[:, c].rearrange("p u f -> p f u")
+                out=h2_tok[:].bitcast(F32)[:, :, c, :, :],
+                in_=h2_turned[:, c].rearrange("p u (s f) -> p s f u", f=F_GROUP),
             )
 
         pieces = cut_into_pieces()
         z_tiles = {}
 
-        def product(index, c):
+        def product(index, passes):
             first, width = pieces[index]
-            if c == 0:
+            if index not in z_tiles:
                 z_tiles[index] = products.tile([P, PASSES, width, F_X, PACK], BF16, name="z", align_bytes=64)
-            shape = [P, width, F_X, PACK]
+            group, inside = divmod(first, F_GROUP)
+            z = z_tiles[index][:, passes]
             nc.vector.tensor_tensor(
-                out=z_tiles[index][:, c],
-                in0=h2_tok[:, c, first : first + width, :].unsqueeze(2).to_broadcast(shape),
-                in1=x0_tok[:, c].unsqueeze(1).to_broadcast(shape),
+                out=z,
+                in0=h2_tok[:, group, passes, inside : inside + width, :].unsqueeze(3).to_broadcast(z.shape),
+                in1=x0_tok[:, passes].unsqueeze(2).to_broadcast(z.shape),
                 op=ALU.mult,
             )
 
+        def products_of(index):
+            if pieces[index][1] == F_GROUP:
+                product(index, slice(0, PASSES))
+            else:
+                for c in range(PASSES):
+                    product(index, slice(c, c + 1))
+
         for c in range(PASSES):
             for index in range(AHEAD):
-                product(index, c)
+                product(index, slice(c, c + 1))
 
         dp_codes = keep.tile([P, PASSES, N], U32, align_bytes=64)
         dp_scales = keep.tile([P, PASSES, N], U8, align_bytes=64)
+        dp = keep.tile([P, PASSES, N, PACK], BF16, align_bytes=64)
         for c in range(PASSES):
             grad_tok = psum.tile([P, N], F32, tag="bank")
             nc.tensor.matmul(
@@ -122,26 +132,24 @@ def tile_cin_pb_v_kernel(tc, h2, x0, W3, b3, pre, grad_out, out):
             )
             sign = keep.tile([P, N, PACK], BF16, name="sign%d" % c)
             nc.scalar.activation(out=sign[:], in_=pre_sb[c][:].rearrange("p j n -> p n j"), func=ACT.Sign)
-            dp = keep.tile([P, N, PACK], BF16, name="dp%d" % c, align_bytes=64)
             nc.vector.scalar_tensor_tensor(
-                out=dp[:],
+                out=dp[:, c],
                 in0=sign[:],
                 scalar=0.0,
                 in1=grad_tok[:].unsqueeze(2).to_broadcast([P, N, PACK]),
                 op0=ALU.max,
                 op1=ALU.mult,
             )
-            nc.vector.quantize_mx(
-                out=dp_codes[:, c, :].bitcast(E5M2X4),
-                scales=dp_scales[:, c, :],
-                in_=dp[:].rearrange("p n j -> p (n j)"),
-            )
+        nc.vector.quantize_mx(
+            out=dp_codes[:].rearrange("p c n -> p (c n)").bitcast(E5M2X4),
+            scales=dp_scales[:].rearrange("p c n -> p (c n)"),
+            in_=dp[:].rearrange("p c n j -> p (c n j)"),
+        )
 
         for index in range(len(pieces)):
             first, width = pieces[index]
             if index + AHEAD < len(pieces):
-                for c in range(PASSES):
-                    product(index + AHEAD, c)
+                products_of(index + AHEAD)
             cols = width * F_X
             z_codes = quantised.tile([P, PASSES, cols], U32, align_bytes=64)
             z_scales = quantised.tile([P, PASSES, cols], U8, align_bytes=64)

@@ -19,19 +19,24 @@ B, F_H, F_X, D, N = 32, 128, 64, 32, 512
 B_PASS = B // PASSES
 TOKENS = B_PASS * D
 F_TILE = P // F_X
-F_GROUP = 8
-AHEAD = 3
+TILES = F_H // F_TILE
+ROWS = PASSES * F_TILE
+WIDEST = 4
+HEAD = 3
+LAST = 3
 
 FLOPS = 2 * B * D * F_H * F_X * N
 BYTES = 2 * (B * F_H * D + B * F_X * D + B * N) + 4 * B * D * N + 4 * F_H * F_X * N
 
 
 def cut_into_pieces():
-    pieces = [(first, F_GROUP) for first in range(0, F_H - F_GROUP, F_GROUP)]
-    first = F_H - F_GROUP
-    for width in (F_GROUP // 2, F_GROUP // 4, F_GROUP // 4):
+    widths = [WIDEST] * (TILES // WIDEST - 2) + [2, 2, 1, 1, 1, 1]
+    pieces = []
+    first = 0
+    for width in widths:
         pieces.append((first, width))
         first += width
+    assert first == TILES
     return pieces
 
 
@@ -39,9 +44,9 @@ def tile_cin_pb_v_kernel(tc, h2, x0, W3, b3, pre, grad_out, out):
     nc = tc.nc
     with ExitStack() as ctx:
         keep = ctx.enter_context(tc.tile_pool(name="keep", bufs=1))
-        products = ctx.enter_context(tc.tile_pool(name="products", bufs=AHEAD + 2))
-        quantised = ctx.enter_context(tc.tile_pool(name="quantised", bufs=4))
-        results = ctx.enter_context(tc.tile_pool(name="results", bufs=4))
+        products = ctx.enter_context(tc.tile_pool(name="products", bufs=HEAD + 1))
+        quantised = ctx.enter_context(tc.tile_pool(name="quantised", bufs=5))
+        results = ctx.enter_context(tc.tile_pool(name="results", bufs=8))
         psum = ctx.enter_context(tc.psum_pool(name="psum", bufs=8))
         ctx.enter_context(tc.manual_schedule())
 
@@ -79,48 +84,74 @@ def tile_cin_pb_v_kernel(tc, h2, x0, W3, b3, pre, grad_out, out):
         x0_turned = psum.tile([P, 2, P], F32, tag="bank")
         for u in range(2):
             nc.tensor.transpose(out=x0_turned[:, u, :], in_=x0_words[:, u, :], identity=identity[:])
-        x0_tok = keep.tile([P, PASSES, F_X, PACK], BF16)
-        nc.scalar.copy(
-            out=x0_tok[:].bitcast(F32),
-            in_=x0_turned[:].rearrange("p u (c g) -> p c g u", c=PASSES),
-        )
+        x0_tok = keep.tile([P, ROWS, F_X, PACK], BF16)
+        x0_tok_words = x0_tok[:].bitcast(F32).rearrange("p (c r) g u -> p c r g u", r=F_TILE)
+        x0_turned_words = x0_turned[:].rearrange("p u (c g) -> p c g u", c=PASSES)
+        nc.scalar.copy(out=x0_tok_words[:, :, 0], in_=x0_turned_words)
+        nc.vector.tensor_copy(out=x0_tok_words[:, :, 1], in_=x0_turned_words)
         h2_words = h2_rows[:].bitcast(F32).rearrange("f (c p u) -> f c u p", c=PASSES, u=2)
         h2_turned = psum.tile([P, PASSES, 2, P], F32, tag="bank")
-        h2_tok = keep.tile([P, F_H // F_GROUP, PASSES, F_GROUP, PACK], BF16)
+        h2_tok = keep.tile([P, TILES, ROWS, PACK], BF16)
+        h2_tok_words = h2_tok[:].bitcast(F32).rearrange("p s (c r) u -> p s c r u", r=F_TILE)
         for c in range(PASSES):
             for u in range(2):
                 nc.tensor.transpose(out=h2_turned[:, c, u, :], in_=h2_words[:, c, u, :], identity=identity[:])
-            nc.vector.tensor_copy(
-                out=h2_tok[:].bitcast(F32)[:, :, c, :, :],
-                in_=h2_turned[:, c].rearrange("p u (s f) -> p s f u", f=F_GROUP),
-            )
+        nc.vector.tensor_copy(
+            out=h2_tok_words[:, :, 0], in_=h2_turned[:, 0].rearrange("p u (s r) -> p s r u", r=F_TILE)
+        )
+        nc.scalar.copy(
+            out=h2_tok_words[:, :, 1], in_=h2_turned[:, 1].rearrange("p u (s r) -> p s r u", r=F_TILE)
+        )
 
         pieces = cut_into_pieces()
         z_tiles = {}
 
-        def product(index, passes):
+        def product(index):
             first, width = pieces[index]
-            if index not in z_tiles:
-                z_tiles[index] = products.tile([P, PASSES, width, F_X, PACK], BF16, name="z", align_bytes=64)
-            group, inside = divmod(first, F_GROUP)
-            z = z_tiles[index][:, passes]
+            z = products.tile([P, width, ROWS, F_X, PACK], BF16, name="z", align_bytes=64)
+            z_tiles[index] = z
             nc.vector.tensor_tensor(
-                out=z,
-                in0=h2_tok[:, group, passes, inside : inside + width, :].unsqueeze(3).to_broadcast(z.shape),
-                in1=x0_tok[:, passes].unsqueeze(2).to_broadcast(z.shape),
+                out=z[:],
+                in0=h2_tok[:, first : first + width].unsqueeze(3).to_broadcast([P, width, ROWS, F_X, PACK]),
+                in1=x0_tok[:].unsqueeze(1).to_broadcast([P, width, ROWS, F_X, PACK]),
                 op=ALU.mult,
             )
 
-        def products_of(index):
-            if pieces[index][1] == F_GROUP:
-                product(index, slice(0, PASSES))
-            else:
+        def finish(index):
+            first, width = pieces[index]
+            z_codes = quantised.tile([P, width, PASSES, P], U32, align_bytes=64)
+            z_scales = quantised.tile([P, width, PASSES, P], U8, align_bytes=64)
+            nc.vector.quantize_mx(
+                out=z_codes[:].rearrange("p i c m -> p (i c m)").bitcast(E4M3X4),
+                scales=z_scales[:].rearrange("p i c m -> p (i c m)"),
+                in_=z_tiles[index][:].rearrange("p i q g j -> p (i q g j)"),
+            )
+            sums = []
+            for i in range(width):
+                acc = psum.tile([P, N], F32, tag="bank")
+                sums.append(acc)
                 for c in range(PASSES):
-                    product(index, slice(c, c + 1))
+                    nc.tensor.matmul_mx(
+                        out=acc[:],
+                        lhsT=z_codes[:, i, c, :].bitcast(E4M3X4),
+                        lhsT_scale=z_scales[:, i, c, :],
+                        rhs=dp_codes[:, c, :].bitcast(E5M2X4),
+                        rhs_scale=dp_scales[:, c, :],
+                        start=(c == 0),
+                        stop=(c == PASSES - 1),
+                    )
+            return sums
 
-        for c in range(PASSES):
-            for index in range(AHEAD):
-                product(index, slice(c, c + 1))
+        def store(index, sums, copy):
+            first, width = pieces[index]
+            result = results.tile([P, width, N], F32)
+            for i in range(width):
+                copy(out=result[:, i, :], in_=sums[i][:])
+            rows = out[first * P : (first + width) * P, :]
+            nc.sync.dma_start(out=rows.rearrange("(i m) n -> m i n", m=P), in_=result[:])
+
+        for index in range(HEAD):
+            product(index)
 
         dp_codes = keep.tile([P, PASSES, N], U32, align_bytes=64)
         dp_scales = keep.tile([P, PASSES, N], U8, align_bytes=64)
@@ -146,32 +177,14 @@ def tile_cin_pb_v_kernel(tc, h2, x0, W3, b3, pre, grad_out, out):
             in_=dp[:].rearrange("p c n j -> p (c n j)"),
         )
 
+        left = []
         for index in range(len(pieces)):
-            first, width = pieces[index]
-            if index + AHEAD < len(pieces):
-                products_of(index + AHEAD)
-            cols = width * F_X
-            z_codes = quantised.tile([P, PASSES, cols], U32, align_bytes=64)
-            z_scales = quantised.tile([P, PASSES, cols], U8, align_bytes=64)
-            nc.vector.quantize_mx(
-                out=z_codes[:].rearrange("p c w -> p (c w)").bitcast(E4M3X4),
-                scales=z_scales[:].rearrange("p c w -> p (c w)"),
-                in_=z_tiles[index][:].rearrange("p c f g j -> p (c f g j)"),
-            )
-            m_tiles = width // F_TILE
-            result = results.tile([P, m_tiles, N], F32)
-            for i in range(m_tiles):
-                acc = psum.tile([P, N], F32, tag="bank")
-                for c in range(PASSES):
-                    nc.tensor.matmul_mx(
-                        out=acc[:],
-                        lhsT=z_codes[:, c, i * P : (i + 1) * P].bitcast(E4M3X4),
-                        lhsT_scale=z_scales[:, c, i * P : (i + 1) * P],
-                        rhs=dp_codes[:, c, :].bitcast(E5M2X4),
-                        rhs_scale=dp_scales[:, c, :],
-                        start=(c == 0),
-                        stop=(c == PASSES - 1),
-                    )
-                nc.scalar.copy(out=result[:, i, :], in_=acc[:])
-            rows = out[first * F_X : (first + width) * F_X, :]
-            nc.sync.dma_start(out=rows.rearrange("(i m) n -> m i n", m=P), in_=result[:])
+            if HEAD - 1 <= index < len(pieces) - 1:
+                product(index + 1)
+            sums = finish(index)
+            if index < len(pieces) - LAST:
+                store(index, sums, nc.scalar.copy)
+            else:
+                left.append((index, sums))
+        for index, sums in left:
+            store(index, sums, nc.vector.tensor_copy)

@@ -47,7 +47,8 @@ def tile_cin_pb_v_kernel(tc, h2, x0, W3, b3, pre, grad_out, out):
         products = ctx.enter_context(tc.tile_pool(name="products", bufs=HEAD + 1))
         quantised = ctx.enter_context(tc.tile_pool(name="quantised", bufs=5))
         results = ctx.enter_context(tc.tile_pool(name="results", bufs=8))
-        psum = ctx.enter_context(tc.psum_pool(name="psum", bufs=8))
+        psum = ctx.enter_context(tc.psum_pool(name="psum", bufs=7))
+        fixed = ctx.enter_context(tc.psum_pool(name="fixed", bufs=1))
         ctx.enter_context(tc.manual_schedule())
 
         h2_rows = keep.tile([P, PASSES * TOKENS], BF16)
@@ -74,6 +75,8 @@ def tile_cin_pb_v_kernel(tc, h2, x0, W3, b3, pre, grad_out, out):
 
         identity = keep.tile([P, P], F32)
         make_identity(nc, identity[:])
+        identity_bf = keep.tile([P, P], BF16)
+        nc.vector.tensor_copy(out=identity_bf[:], in_=identity[:])
         spread = keep.tile([P, B, P // B_PASS], BF16)
         nc.vector.tensor_copy(
             out=spread[:], in_=identity[:, 0:B].unsqueeze(2).to_broadcast([P, B, P // B_PASS])
@@ -89,19 +92,24 @@ def tile_cin_pb_v_kernel(tc, h2, x0, W3, b3, pre, grad_out, out):
         x0_turned_words = x0_turned[:].rearrange("p u (c g) -> p c g u", c=PASSES)
         nc.scalar.copy(out=x0_tok_words[:, :, 0], in_=x0_turned_words)
         nc.vector.tensor_copy(out=x0_tok_words[:, :, 1], in_=x0_turned_words)
+        x0_psum = fixed.tile([P, ROWS, F_X, PACK], BF16)
+        for c in range(PASSES):
+            rows_c = slice(c * F_TILE, (c + 1) * F_TILE)
+            nc.tensor.matmul(
+                out=x0_psum[:, rows_c].rearrange("p q g j -> p (q g j)"),
+                lhsT=identity_bf[:],
+                rhs=x0_tok[:, rows_c].rearrange("p q g j -> p (q g j)"),
+                start=True,
+                stop=True,
+            )
         h2_words = h2_rows[:].bitcast(F32).rearrange("f (c p u) -> f c u p", c=PASSES, u=2)
-        h2_turned = psum.tile([P, PASSES, 2, P], F32, tag="bank")
         h2_tok = keep.tile([P, TILES, ROWS, PACK], BF16)
         h2_tok_words = h2_tok[:].bitcast(F32).rearrange("p s (c r) u -> p s c r u", r=F_TILE)
-        for c in range(PASSES):
+        for c, copy in enumerate((nc.vector.tensor_copy, nc.scalar.copy)):
+            h2_turned = psum.tile([P, 2, P], F32, tag="bank")
             for u in range(2):
-                nc.tensor.transpose(out=h2_turned[:, c, u, :], in_=h2_words[:, c, u, :], identity=identity[:])
-        nc.vector.tensor_copy(
-            out=h2_tok_words[:, :, 0], in_=h2_turned[:, 0].rearrange("p u (s r) -> p s r u", r=F_TILE)
-        )
-        nc.scalar.copy(
-            out=h2_tok_words[:, :, 1], in_=h2_turned[:, 1].rearrange("p u (s r) -> p s r u", r=F_TILE)
-        )
+                nc.tensor.transpose(out=h2_turned[:, u, :], in_=h2_words[:, c, u, :], identity=identity[:])
+            copy(out=h2_tok_words[:, :, c], in_=h2_turned[:].rearrange("p u (s r) -> p s r u", r=F_TILE))
 
         pieces = cut_into_pieces()
         z_tiles = {}
@@ -113,7 +121,7 @@ def tile_cin_pb_v_kernel(tc, h2, x0, W3, b3, pre, grad_out, out):
             nc.vector.tensor_tensor(
                 out=z[:],
                 in0=h2_tok[:, first : first + width].unsqueeze(3).to_broadcast([P, width, ROWS, F_X, PACK]),
-                in1=x0_tok[:].unsqueeze(1).to_broadcast([P, width, ROWS, F_X, PACK]),
+                in1=x0_psum[:].unsqueeze(1).to_broadcast([P, width, ROWS, F_X, PACK]),
                 op=ALU.mult,
             )
 

@@ -22,7 +22,9 @@ F_TILE = P // F_X
 TILES = F_H // F_TILE
 ROWS = PASSES * F_TILE
 WIDEST = 4
-HEAD = 3
+HEAD = 4
+N_BANK = 256
+N_PLAIN = 128
 LAST = 3
 
 FLOPS = 2 * B * D * F_H * F_X * N
@@ -165,20 +167,28 @@ def tile_cin_pb_v_kernel(tc, h2, x0, W3, b3, pre, grad_out, out):
         dp_scales = keep.tile([P, PASSES, N], U8, align_bytes=64)
         dp = keep.tile([P, PASSES, N, PACK], BF16, align_bytes=64)
         for c in range(PASSES):
-            grad_tok = psum.tile([P, N], F32, tag="bank")
-            nc.tensor.matmul(
-                out=grad_tok[:], lhsT=spread_cols[:, c * P : (c + 1) * P], rhs=grad_rows[:], start=True, stop=True
-            )
             sign = keep.tile([P, N, PACK], BF16, name="sign%d" % c)
             nc.scalar.activation(out=sign[:], in_=pre_sb[c][:].rearrange("p j n -> p n j"), func=ACT.Sign)
-            nc.vector.scalar_tensor_tensor(
-                out=dp[:, c],
-                in0=sign[:],
-                scalar=0.0,
-                in1=grad_tok[:].unsqueeze(2).to_broadcast([P, N, PACK]),
-                op0=ALU.max,
-                op1=ALU.mult,
-            )
+            mask = keep.tile([P, N, PACK], BF16, name="mask%d" % c)
+            nc.scalar.activation(out=mask[:], in_=sign[:], func=ACT.Relu)
+            for first in range(0, N, N_BANK):
+                grad_tok = psum.tile([P, N_BANK, PACK], BF16, tag="bank")
+                for inside in range(0, N_BANK, N_PLAIN):
+                    nc.tensor.matmul(
+                        out=grad_tok[:, inside : inside + N_PLAIN, :].rearrange("p n j -> p (n j)"),
+                        lhsT=spread_cols[:, c * P : (c + 1) * P],
+                        rhs=grad_rows[:, first + inside : first + inside + N_PLAIN]
+                        .unsqueeze(2)
+                        .to_broadcast([P, N_PLAIN, PACK]),
+                        start=True,
+                        stop=True,
+                    )
+                nc.vector.tensor_tensor(
+                    out=dp[:, c, first : first + N_BANK, :],
+                    in0=mask[:, first : first + N_BANK, :],
+                    in1=grad_tok[:],
+                    op=ALU.mult,
+                )
         nc.vector.quantize_mx(
             out=dp_codes[:].rearrange("p c n -> p (c n)").bitcast(E5M2X4),
             scales=dp_scales[:].rearrange("p c n -> p (c n)"),

@@ -22,7 +22,8 @@ F_TILE = P // F_X
 TILES = F_H // F_TILE
 ROWS = PASSES * F_TILE
 WIDEST = 4
-HEAD = 4
+FULL = 2 * WIDEST
+HEAD = 3
 N_BANK = 256
 N_PLAIN = 128
 LAST = 3
@@ -32,11 +33,11 @@ BYTES = 2 * (B * F_H * D + B * F_X * D + B * N) + 4 * B * D * N + 4 * F_H * F_X 
 
 
 def cut_into_pieces():
-    widths = [WIDEST] * (TILES // WIDEST - 2) + [2, 2, 1, 1, 1, 1]
+    widths = [FULL] * (TILES // FULL - 1) + [2, 2, 1, 1, 1, 1]
     pieces = []
     first = 0
-    for width in widths:
-        pieces.append((first, width))
+    for index, width in enumerate(widths):
+        pieces.append((first, width, 1 if width == FULL and index != HEAD else 0))
         first += width
     assert first == TILES
     return pieces
@@ -46,8 +47,8 @@ def tile_cin_pb_v_kernel(tc, h2, x0, W3, b3, pre, grad_out, out):
     nc = tc.nc
     with ExitStack() as ctx:
         keep = ctx.enter_context(tc.tile_pool(name="keep", bufs=1))
-        products = ctx.enter_context(tc.tile_pool(name="products", bufs=HEAD + 1))
-        quantised = ctx.enter_context(tc.tile_pool(name="quantised", bufs=5))
+        products = ctx.enter_context(tc.tile_pool(name="products", bufs=HEAD))
+        quantised = ctx.enter_context(tc.tile_pool(name="quantised", bufs=6))
         results = ctx.enter_context(tc.tile_pool(name="results", bufs=8))
         psum = ctx.enter_context(tc.psum_pool(name="psum", bufs=7))
         fixed = ctx.enter_context(tc.psum_pool(name="fixed", bufs=1))
@@ -117,24 +118,27 @@ def tile_cin_pb_v_kernel(tc, h2, x0, W3, b3, pre, grad_out, out):
         z_tiles = {}
 
         def product(index):
-            first, width = pieces[index]
+            first, width, helped = pieces[index]
             z = products.tile([P, width, ROWS, F_X, PACK], BF16, name="z", align_bytes=64)
             z_tiles[index] = z
-            nc.vector.tensor_tensor(
-                out=z[:],
-                in0=h2_tok[:, first : first + width].unsqueeze(3).to_broadcast([P, width, ROWS, F_X, PACK]),
-                in1=x0_psum[:].unsqueeze(1).to_broadcast([P, width, ROWS, F_X, PACK]),
-                op=ALU.mult,
-            )
+            own = width - helped
+            for engine, x0_there, start, count in ((nc.vector, x0_psum, 0, own), (nc.gpsimd, x0_tok, own, helped)):
+                if count > 0:
+                    shape = [P, count, ROWS, F_X, PACK]
+                    engine.tensor_tensor(
+                        out=z[:, start : start + count],
+                        in0=h2_tok[:, first + start : first + start + count].unsqueeze(3).to_broadcast(shape),
+                        in1=x0_there[:].unsqueeze(1).to_broadcast(shape),
+                        op=ALU.mult,
+                    )
 
-        def finish(index):
-            first, width = pieces[index]
+        def finish(index, start, width):
             z_codes = quantised.tile([P, width, PASSES, P], U32, align_bytes=64)
             z_scales = quantised.tile([P, width, PASSES, P], U8, align_bytes=64)
             nc.vector.quantize_mx(
                 out=z_codes[:].rearrange("p i c m -> p (i c m)").bitcast(E4M3X4),
                 scales=z_scales[:].rearrange("p i c m -> p (i c m)"),
-                in_=z_tiles[index][:].rearrange("p i q g j -> p (i q g j)"),
+                in_=z_tiles[index][:, start : start + width].rearrange("p i q g j -> p (i q g j)"),
             )
             sums = []
             for i in range(width):
@@ -152,8 +156,8 @@ def tile_cin_pb_v_kernel(tc, h2, x0, W3, b3, pre, grad_out, out):
                     )
             return sums
 
-        def store(index, sums, copy):
-            first, width = pieces[index]
+        def store(first, sums, copy):
+            width = len(sums)
             result = results.tile([P, width, N], F32)
             for i in range(width):
                 copy(out=result[:, i, :], in_=sums[i][:])
@@ -199,10 +203,12 @@ def tile_cin_pb_v_kernel(tc, h2, x0, W3, b3, pre, grad_out, out):
         for index in range(len(pieces)):
             if HEAD - 1 <= index < len(pieces) - 1:
                 product(index + 1)
-            sums = finish(index)
-            if index < len(pieces) - LAST:
-                store(index, sums, nc.scalar.copy)
-            else:
-                left.append((index, sums))
-        for index, sums in left:
-            store(index, sums, nc.vector.tensor_copy)
+            first, width, helped = pieces[index]
+            for start in range(0, width, WIDEST):
+                sums = finish(index, start, min(WIDEST, width))
+                if index < len(pieces) - LAST:
+                    store(first + start, sums, nc.scalar.copy)
+                else:
+                    left.append((first + start, sums))
+        for first, sums in left:
+            store(first, sums, nc.vector.tensor_copy)

@@ -23,7 +23,8 @@ TILES = F_H // F_TILE
 ROWS = PASSES * F_TILE
 WIDEST = 4
 FULL = 2 * WIDEST
-HEAD = 3
+HEAD = 2
+F_HEAD = HEAD * FULL * F_TILE
 N_BANK = 256
 N_PLAIN = 128
 LAST = 3
@@ -37,7 +38,13 @@ def cut_into_pieces():
     pieces = []
     first = 0
     for index, width in enumerate(widths):
-        pieces.append((first, width, 1 if width == FULL and index != HEAD else 0))
+        if index < HEAD:
+            helped = 2
+        elif index == HEAD or index > TILES // FULL - 1:
+            helped = 0
+        else:
+            helped = 1
+        pieces.append((first, width, helped))
         first += width
     assert first == TILES
     return pieces
@@ -47,34 +54,46 @@ def tile_cin_pb_v_kernel(tc, h2, x0, W3, b3, pre, grad_out, out):
     nc = tc.nc
     with ExitStack() as ctx:
         keep = ctx.enter_context(tc.tile_pool(name="keep", bufs=1))
-        products = ctx.enter_context(tc.tile_pool(name="products", bufs=HEAD))
+        products = ctx.enter_context(tc.tile_pool(name="products", bufs=3))
         quantised = ctx.enter_context(tc.tile_pool(name="quantised", bufs=6))
         results = ctx.enter_context(tc.tile_pool(name="results", bufs=8))
         psum = ctx.enter_context(tc.psum_pool(name="psum", bufs=7))
         fixed = ctx.enter_context(tc.psum_pool(name="fixed", bufs=1))
         ctx.enter_context(tc.manual_schedule())
 
-        h2_rows = keep.tile([P, PASSES * TOKENS], BF16)
-        x0_rows = keep.tile([P, TOKENS], BF16)
         grad_rows = keep.tile([P, N], BF16)
-        nc.vector.memset(grad_rows[:], 0.0)
-        nc.scalar.dma_start(out=grad_rows[0:B, :], in_=grad_out)
+        nc.sync.dma_start(out=grad_rows[0:B, :], in_=grad_out)
+        nc.vector.memset(grad_rows[B : 2 * B, :], 0.0)
+        nc.vector.memset(grad_rows[2 * B : P, :], 0.0)
+        x0_rows = keep.tile([P, TOKENS], BF16)
         for c in range(PASSES):
             nc.sync.dma_start(
                 out=x0_rows[c * F_X : (c + 1) * F_X, :].rearrange("g (b d) -> g b d", d=D),
                 in_=x0[c * B_PASS : (c + 1) * B_PASS].rearrange("b g d -> g b d"),
             )
-        for c in range(PASSES):
-            nc.sync.dma_start(
-                out=h2_rows[:, c * TOKENS : (c + 1) * TOKENS].rearrange("f (b d) -> f b d", d=D),
-                in_=h2[c * B_PASS : (c + 1) * B_PASS].rearrange("b f d -> f b d"),
-            )
+        head_rows = keep.tile([P, PASSES * TOKENS], BF16)
+        nc.sync.dma_start(
+            out=head_rows[0:F_HEAD, :].rearrange("f (b d) -> f b d", d=D),
+            in_=h2[:, 0:F_HEAD, :].rearrange("b f d -> f b d"),
+        )
+        nc.vector.memset(head_rows[F_HEAD : 2 * F_HEAD, :], 0.0)
+        nc.vector.memset(head_rows[2 * F_HEAD : P, :], 0.0)
         pre_rows = pre.rearrange("b d n -> (b d) n").rearrange("(c p j) n -> c p j n", c=PASSES, j=PACK)
         pre_sb = []
         for c in range(PASSES):
             pre_c = keep.tile([P, PACK, N], F32, name="pre_sb%d" % c)
             nc.sync.dma_start(out=pre_c[:], in_=pre_rows[c])
             pre_sb.append(pre_c)
+        h2_rows = keep.tile([P, PASSES * TOKENS], BF16)
+        for c in range(PASSES):
+            nc.sync.dma_start(
+                out=h2_rows[:, c * TOKENS : (c + 1) * TOKENS].rearrange("f (b d) -> f b d", d=D),
+                in_=h2[c * B_PASS : (c + 1) * B_PASS].rearrange("b f d -> f b d"),
+            )
+
+        warm = keep.tile([P, 2], F32)
+        nc.vector.memset(warm[:], 0.0)
+        nc.scalar.activation(out=warm[:, 1:2], in_=warm[:, 0:1], func=ACT.Sign)
 
         identity = keep.tile([P, P], F32)
         make_identity(nc, identity[:])
@@ -90,29 +109,34 @@ def tile_cin_pb_v_kernel(tc, h2, x0, W3, b3, pre, grad_out, out):
         x0_turned = psum.tile([P, 2, P], F32, tag="bank")
         for u in range(2):
             nc.tensor.transpose(out=x0_turned[:, u, :], in_=x0_words[:, u, :], identity=identity[:])
-        x0_tok = keep.tile([P, ROWS, F_X, PACK], BF16)
-        x0_tok_words = x0_tok[:].bitcast(F32).rearrange("p (c r) g u -> p c r g u", r=F_TILE)
-        x0_turned_words = x0_turned[:].rearrange("p u (c g) -> p c g u", c=PASSES)
-        nc.scalar.copy(out=x0_tok_words[:, :, 0], in_=x0_turned_words)
-        nc.vector.tensor_copy(out=x0_tok_words[:, :, 1], in_=x0_turned_words)
+        x0_tok = keep.tile([P, PASSES, F_X, PACK], BF16)
+        nc.vector.tensor_copy(
+            out=x0_tok[:].bitcast(F32), in_=x0_turned[:].rearrange("p u (c g) -> p c g u", c=PASSES)
+        )
+        h2_tok = keep.tile([P, TILES, ROWS, PACK], BF16)
+        h2_tok_words = h2_tok[:].bitcast(F32).rearrange("p s (c r) u -> p s c r u", r=F_TILE)
+
+        def turn_h2(rows, c, fields, copy):
+            words = rows[:].bitcast(F32).rearrange("f (c p u) -> f c u p", c=PASSES, u=2)
+            turned = psum.tile([P, 2, P], F32, tag="bank")
+            for u in range(2):
+                nc.tensor.transpose(out=turned[:, u, :], in_=words[:, c, u, :], identity=identity[:])
+            copy(
+                out=h2_tok_words[:, fields.start // F_TILE : fields.stop // F_TILE, c],
+                in_=turned[:, :, fields].rearrange("p u (s r) -> p s r u", r=F_TILE),
+            )
+
+        for c in range(PASSES):
+            turn_h2(head_rows, c, slice(0, F_HEAD), nc.vector.tensor_copy)
         x0_psum = fixed.tile([P, ROWS, F_X, PACK], BF16)
         for c in range(PASSES):
-            rows_c = slice(c * F_TILE, (c + 1) * F_TILE)
             nc.tensor.matmul(
-                out=x0_psum[:, rows_c].rearrange("p q g j -> p (q g j)"),
+                out=x0_psum[:, c * F_TILE : (c + 1) * F_TILE].rearrange("p r g j -> p (r g j)"),
                 lhsT=identity_bf[:],
-                rhs=x0_tok[:, rows_c].rearrange("p q g j -> p (q g j)"),
+                rhs=x0_tok[:, c].rearrange("p g j -> p (g j)").unsqueeze(1).to_broadcast([P, F_TILE, F_X * PACK]),
                 start=True,
                 stop=True,
             )
-        h2_words = h2_rows[:].bitcast(F32).rearrange("f (c p u) -> f c u p", c=PASSES, u=2)
-        h2_tok = keep.tile([P, TILES, ROWS, PACK], BF16)
-        h2_tok_words = h2_tok[:].bitcast(F32).rearrange("p s (c r) u -> p s c r u", r=F_TILE)
-        for c, copy in enumerate((nc.vector.tensor_copy, nc.scalar.copy)):
-            h2_turned = psum.tile([P, 2, P], F32, tag="bank")
-            for u in range(2):
-                nc.tensor.transpose(out=h2_turned[:, u, :], in_=h2_words[:, c, u, :], identity=identity[:])
-            copy(out=h2_tok_words[:, :, c], in_=h2_turned[:].rearrange("p u (s r) -> p s r u", r=F_TILE))
 
         pieces = cut_into_pieces()
         z_tiles = {}
@@ -122,15 +146,21 @@ def tile_cin_pb_v_kernel(tc, h2, x0, W3, b3, pre, grad_out, out):
             z = products.tile([P, width, ROWS, F_X, PACK], BF16, name="z", align_bytes=64)
             z_tiles[index] = z
             own = width - helped
-            for engine, x0_there, start, count in ((nc.vector, x0_psum, 0, own), (nc.gpsimd, x0_tok, own, helped)):
-                if count > 0:
-                    shape = [P, count, ROWS, F_X, PACK]
-                    engine.tensor_tensor(
-                        out=z[:, start : start + count],
-                        in0=h2_tok[:, first + start : first + start + count].unsqueeze(3).to_broadcast(shape),
-                        in1=x0_there[:].unsqueeze(1).to_broadcast(shape),
-                        op=ALU.mult,
-                    )
+            shape = [P, own, ROWS, F_X, PACK]
+            nc.vector.tensor_tensor(
+                out=z[:, 0:own],
+                in0=h2_tok[:, first : first + own].unsqueeze(3).to_broadcast(shape),
+                in1=x0_psum[:].unsqueeze(1).to_broadcast(shape),
+                op=ALU.mult,
+            )
+            shape = [P, PASSES, F_TILE, F_X, PACK]
+            for i in range(own, width):
+                nc.gpsimd.tensor_tensor(
+                    out=z[:, i].rearrange("p (c r) g j -> p c r g j", r=F_TILE),
+                    in0=h2_tok[:, first + i].rearrange("p (c r) j -> p c r j", r=F_TILE).unsqueeze(3).to_broadcast(shape),
+                    in1=x0_tok[:].unsqueeze(2).to_broadcast(shape),
+                    op=ALU.mult,
+                )
 
         def finish(index, start, width):
             z_codes = quantised.tile([P, width, PASSES, P], U32, align_bytes=64)
@@ -170,11 +200,17 @@ def tile_cin_pb_v_kernel(tc, h2, x0, W3, b3, pre, grad_out, out):
         dp_codes = keep.tile([P, PASSES, N], U32, align_bytes=64)
         dp_scales = keep.tile([P, PASSES, N], U8, align_bytes=64)
         dp = keep.tile([P, PASSES, N, PACK], BF16, align_bytes=64)
+        sign_of = []
+        mask_of = []
         for c in range(PASSES):
             sign = keep.tile([P, N, PACK], BF16, name="sign%d" % c)
             nc.scalar.activation(out=sign[:], in_=pre_sb[c][:].rearrange("p j n -> p n j"), func=ACT.Sign)
+            sign_of.append(sign)
             mask = keep.tile([P, N, PACK], BF16, name="mask%d" % c)
-            nc.scalar.activation(out=mask[:], in_=sign[:], func=ACT.Relu)
+            mask_of.append(mask)
+        nc.scalar.activation(out=mask_of[0][:], in_=sign_of[0][:], func=ACT.Relu)
+        nc.vector.tensor_scalar_max(out=mask_of[1][:], in0=sign_of[1][:], scalar1=0.0)
+        for c in reversed(range(PASSES)):
             for first in range(0, N, N_BANK):
                 grad_tok = psum.tile([P, N_BANK, PACK], BF16, tag="bank")
                 for inside in range(0, N_BANK, N_PLAIN):
@@ -189,10 +225,12 @@ def tile_cin_pb_v_kernel(tc, h2, x0, W3, b3, pre, grad_out, out):
                     )
                 nc.vector.tensor_tensor(
                     out=dp[:, c, first : first + N_BANK, :],
-                    in0=mask[:, first : first + N_BANK, :],
+                    in0=mask_of[c][:, first : first + N_BANK, :],
                     in1=grad_tok[:],
                     op=ALU.mult,
                 )
+        for c in range(PASSES):
+            turn_h2(h2_rows, c, slice(F_HEAD, F_H), nc.scalar.copy)
         nc.vector.quantize_mx(
             out=dp_codes[:].rearrange("p c n -> p (c n)").bitcast(E5M2X4),
             scales=dp_scales[:].rearrange("p c n -> p (c n)"),

@@ -38,7 +38,7 @@ def cut_into_pieces():
     pieces = []
     first = 0
     for index, width in enumerate(widths):
-        if index < HEAD:
+        if index == 0:
             helped = 2
         elif index == HEAD or index > TILES // FULL - 1:
             helped = 0

@@ -23,8 +23,8 @@ TILES = F_H // F_TILE
 ROWS = PASSES * F_TILE
 WIDEST = 4
 FULL = 2 * WIDEST
-HEAD = 2
-F_HEAD = HEAD * FULL * F_TILE
+HEAD = 3
+F_HALF = F_H // 2
 N_BANK = 256
 N_PLAIN = 128
 LAST = 3
@@ -71,25 +71,27 @@ def tile_cin_pb_v_kernel(tc, h2, x0, W3, b3, pre, grad_out, out):
                 out=x0_rows[c * F_X : (c + 1) * F_X, :].rearrange("g (b d) -> g b d", d=D),
                 in_=x0[c * B_PASS : (c + 1) * B_PASS].rearrange("b g d -> g b d"),
             )
-        head_rows = keep.tile([P, PASSES * TOKENS], BF16)
-        nc.sync.dma_start(
-            out=head_rows[0:F_HEAD, :].rearrange("f (b d) -> f b d", d=D),
-            in_=h2[:, 0:F_HEAD, :].rearrange("b f d -> f b d"),
-        )
-        nc.vector.memset(head_rows[F_HEAD : 2 * F_HEAD, :], 0.0)
-        nc.vector.memset(head_rows[2 * F_HEAD : P, :], 0.0)
+        h2_rows = []
+        for half in range(2):
+            rows = keep.tile([P, PASSES * TOKENS], BF16, name="h2_rows%d" % half)
+            h2_rows.append(rows)
+            nc.vector.memset(rows[(1 - half) * F_HALF : (2 - half) * F_HALF, :], 0.0)
+
+        def load_h2(half):
+            fields = slice(half * F_HALF, (half + 1) * F_HALF)
+            nc.sync.dma_start(
+                out=h2_rows[half][fields, :].rearrange("f (b d) -> f b d", d=D),
+                in_=h2[:, fields, :].rearrange("b f d -> f b d"),
+            )
+
+        load_h2(0)
         pre_rows = pre.rearrange("b d n -> (b d) n").rearrange("(c p j) n -> c p j n", c=PASSES, j=PACK)
         pre_sb = []
         for c in range(PASSES):
             pre_c = keep.tile([P, PACK, N], F32, name="pre_sb%d" % c)
             nc.sync.dma_start(out=pre_c[:], in_=pre_rows[c])
             pre_sb.append(pre_c)
-        h2_rows = keep.tile([P, PASSES * TOKENS], BF16)
-        for c in range(PASSES):
-            nc.sync.dma_start(
-                out=h2_rows[:, c * TOKENS : (c + 1) * TOKENS].rearrange("f (b d) -> f b d", d=D),
-                in_=h2[c * B_PASS : (c + 1) * B_PASS].rearrange("b f d -> f b d"),
-            )
+        load_h2(1)
 
         warm = keep.tile([P, 2], F32)
         nc.vector.memset(warm[:], 0.0)
@@ -127,7 +129,7 @@ def tile_cin_pb_v_kernel(tc, h2, x0, W3, b3, pre, grad_out, out):
             )
 
         for c in range(PASSES):
-            turn_h2(head_rows, c, slice(0, F_HEAD), nc.vector.tensor_copy)
+            turn_h2(h2_rows[0], c, slice(0, F_HALF), nc.vector.tensor_copy)
         x0_psum = fixed.tile([P, ROWS, F_X, PACK], BF16)
         for c in range(PASSES):
             nc.tensor.matmul(
@@ -200,17 +202,14 @@ def tile_cin_pb_v_kernel(tc, h2, x0, W3, b3, pre, grad_out, out):
         dp_codes = keep.tile([P, PASSES, N], U32, align_bytes=64)
         dp_scales = keep.tile([P, PASSES, N], U8, align_bytes=64)
         dp = keep.tile([P, PASSES, N, PACK], BF16, align_bytes=64)
-        sign_of = []
         mask_of = []
         for c in range(PASSES):
             sign = keep.tile([P, N, PACK], BF16, name="sign%d" % c)
             nc.scalar.activation(out=sign[:], in_=pre_sb[c][:].rearrange("p j n -> p n j"), func=ACT.Sign)
-            sign_of.append(sign)
             mask = keep.tile([P, N, PACK], BF16, name="mask%d" % c)
+            nc.scalar.activation(out=mask[:], in_=sign[:], func=ACT.Relu)
             mask_of.append(mask)
-        nc.scalar.activation(out=mask_of[0][:], in_=sign_of[0][:], func=ACT.Relu)
-        nc.vector.tensor_scalar_max(out=mask_of[1][:], in0=sign_of[1][:], scalar1=0.0)
-        for c in reversed(range(PASSES)):
+        for c in range(PASSES):
             for first in range(0, N, N_BANK):
                 grad_tok = psum.tile([P, N_BANK, PACK], BF16, tag="bank")
                 for inside in range(0, N_BANK, N_PLAIN):
@@ -230,7 +229,7 @@ def tile_cin_pb_v_kernel(tc, h2, x0, W3, b3, pre, grad_out, out):
                     op=ALU.mult,
                 )
         for c in range(PASSES):
-            turn_h2(h2_rows, c, slice(F_HEAD, F_H), nc.scalar.copy)
+            turn_h2(h2_rows[1], c, slice(F_HALF, F_H), nc.scalar.copy)
         nc.vector.quantize_mx(
             out=dp_codes[:].rearrange("p c n -> p (c n)").bitcast(E5M2X4),
             scales=dp_scales[:].rearrange("p c n -> p (c n)"),

@@ -61,13 +61,9 @@ def tile_cin_pb_v_kernel(tc, h2, x0, W3, b3, pre, grad_out, out):
         fixed = ctx.enter_context(tc.psum_pool(name="fixed", bufs=1))
         ctx.enter_context(tc.manual_schedule())
 
-        grad_rows = keep.tile([P, N], BF16)
-        nc.sync.dma_start(out=grad_rows[0:B, :], in_=grad_out)
-        nc.vector.memset(grad_rows[B : 2 * B, :], 0.0)
-        nc.vector.memset(grad_rows[2 * B : P, :], 0.0)
         x0_rows = keep.tile([P, TOKENS], BF16)
-        for c in range(PASSES):
-            nc.sync.dma_start(
+        for c, queue in enumerate((nc.sync, nc.scalar)):
+            queue.dma_start(
                 out=x0_rows[c * F_X : (c + 1) * F_X, :].rearrange("g (b d) -> g b d", d=D),
                 in_=x0[c * B_PASS : (c + 1) * B_PASS].rearrange("b g d -> g b d"),
             )
@@ -77,21 +73,25 @@ def tile_cin_pb_v_kernel(tc, h2, x0, W3, b3, pre, grad_out, out):
             h2_rows.append(rows)
             nc.vector.memset(rows[(1 - half) * F_HALF : (2 - half) * F_HALF, :], 0.0)
 
-        def load_h2(half):
-            fields = slice(half * F_HALF, (half + 1) * F_HALF)
-            nc.sync.dma_start(
+        def load_h2(queue, half, fields):
+            queue.dma_start(
                 out=h2_rows[half][fields, :].rearrange("f (b d) -> f b d", d=D),
                 in_=h2[:, fields, :].rearrange("b f d -> f b d"),
             )
 
-        load_h2(0)
+        load_h2(nc.sync, 0, slice(0, F_HALF // 2))
+        load_h2(nc.scalar, 0, slice(F_HALF // 2, F_HALF))
+        grad_rows = keep.tile([P, N], BF16)
+        nc.scalar.dma_start(out=grad_rows[0:B, :], in_=grad_out)
+        nc.vector.memset(grad_rows[B : 2 * B, :], 0.0)
+        nc.vector.memset(grad_rows[2 * B : P, :], 0.0)
         pre_rows = pre.rearrange("b d n -> (b d) n").rearrange("(c p j) n -> c p j n", c=PASSES, j=PACK)
         pre_sb = []
         for c in range(PASSES):
             pre_c = keep.tile([P, PACK, N], F32, name="pre_sb%d" % c)
-            nc.sync.dma_start(out=pre_c[:], in_=pre_rows[c])
+            nc.scalar.dma_start(out=pre_c[:], in_=pre_rows[c])
             pre_sb.append(pre_c)
-        load_h2(1)
+        load_h2(nc.scalar, 1, slice(F_HALF, F_H))
 
         warm = keep.tile([P, 2], F32)
         nc.vector.memset(warm[:], 0.0)

@@ -18,13 +18,11 @@ PASSES = 2
 B, F_H, F_X, D, N = 32, 128, 64, 32, 512
 B_PASS = B // PASSES
 TOKENS = B_PASS * D
-F_TILE = P // F_X
-TILES = F_H // F_TILE
-ROWS = PASSES * F_TILE
+TILES = F_X
 WIDEST = 4
 FULL = 2 * WIDEST
 HEAD = 3
-F_HALF = F_H // 2
+EARLY = 2
 N_BANK = 256
 N_PLAIN = 128
 LAST = 3
@@ -68,19 +66,18 @@ def tile_cin_pb_v_kernel(tc, h2, x0, W3, b3, pre, grad_out, out):
                 in_=x0[c * B_PASS : (c + 1) * B_PASS].rearrange("b g d -> g b d"),
             )
         h2_rows = []
-        for half in range(2):
-            rows = keep.tile([P, PASSES * TOKENS], BF16, name="h2_rows%d" % half)
+        for c in range(PASSES):
+            rows = keep.tile([P, TOKENS], BF16, name="h2_rows%d" % c)
             h2_rows.append(rows)
-            nc.vector.memset(rows[(1 - half) * F_HALF : (2 - half) * F_HALF, :], 0.0)
 
-        def load_h2(queue, half, fields):
+        def load_h2(queue, c, fields):
             queue.dma_start(
-                out=h2_rows[half][fields, :].rearrange("f (b d) -> f b d", d=D),
-                in_=h2[:, fields, :].rearrange("b f d -> f b d"),
+                out=h2_rows[c][fields, :].rearrange("f (b d) -> f b d", d=D),
+                in_=h2[c * B_PASS : (c + 1) * B_PASS, fields, :].rearrange("b f d -> f b d"),
             )
 
-        load_h2(nc.sync, 0, slice(0, F_HALF // 2))
-        load_h2(nc.scalar, 0, slice(F_HALF // 2, F_HALF))
+        load_h2(nc.sync, 0, slice(0, F_H // 2))
+        load_h2(nc.scalar, 0, slice(F_H // 2, F_H))
         grad_rows = keep.tile([P, N], BF16)
         nc.scalar.dma_start(out=grad_rows[0:B, :], in_=grad_out)
         nc.vector.memset(grad_rows[B : 2 * B, :], 0.0)
@@ -91,7 +88,8 @@ def tile_cin_pb_v_kernel(tc, h2, x0, W3, b3, pre, grad_out, out):
             pre_c = keep.tile([P, PACK, N], F32, name="pre_sb%d" % c)
             nc.scalar.dma_start(out=pre_c[:], in_=pre_rows[c])
             pre_sb.append(pre_c)
-        load_h2(nc.scalar, 1, slice(F_HALF, F_H))
+            if c == 0:
+                load_h2(nc.scalar, 1, slice(0, F_H))
 
         warm = keep.tile([P, 2], F32)
         nc.vector.memset(warm[:], 0.0)
@@ -99,8 +97,6 @@ def tile_cin_pb_v_kernel(tc, h2, x0, W3, b3, pre, grad_out, out):
 
         identity = keep.tile([P, P], F32)
         make_identity(nc, identity[:])
-        identity_bf = keep.tile([P, P], BF16)
-        nc.vector.tensor_copy(out=identity_bf[:], in_=identity[:])
         spread = keep.tile([P, B, P // B_PASS], BF16)
         nc.vector.tensor_copy(
             out=spread[:], in_=identity[:, 0:B].unsqueeze(2).to_broadcast([P, B, P // B_PASS])
@@ -111,56 +107,73 @@ def tile_cin_pb_v_kernel(tc, h2, x0, W3, b3, pre, grad_out, out):
         x0_turned = psum.tile([P, 2, P], F32, tag="bank")
         for u in range(2):
             nc.tensor.transpose(out=x0_turned[:, u, :], in_=x0_words[:, u, :], identity=identity[:])
-        x0_tok = keep.tile([P, PASSES, F_X, PACK], BF16)
+        x0_tok = keep.tile([P, F_X, PASSES, PACK], BF16)
         nc.vector.tensor_copy(
-            out=x0_tok[:].bitcast(F32), in_=x0_turned[:].rearrange("p u (c g) -> p c g u", c=PASSES)
+            out=x0_tok[:].bitcast(F32), in_=x0_turned[:].rearrange("p u (c g) -> p g c u", c=PASSES)
         )
-        h2_tok = keep.tile([P, TILES, ROWS, PACK], BF16)
-        h2_tok_words = h2_tok[:].bitcast(F32).rearrange("p s (c r) u -> p s c r u", r=F_TILE)
 
-        def turn_h2(rows, c, fields, copy):
-            words = rows[:].bitcast(F32).rearrange("f (c p u) -> f c u p", c=PASSES, u=2)
-            turned = psum.tile([P, 2, P], F32, tag="bank")
+        def turn_h2(c, turned):
+            words = h2_rows[c][:].bitcast(F32).rearrange("f (p u) -> f u p", u=2)
             for u in range(2):
-                nc.tensor.transpose(out=turned[:, u, :], in_=words[:, c, u, :], identity=identity[:])
-            copy(
-                out=h2_tok_words[:, fields.start // F_TILE : fields.stop // F_TILE, c],
-                in_=turned[:, :, fields].rearrange("p u (s r) -> p s r u", r=F_TILE),
-            )
+                nc.tensor.transpose(out=turned[:, :, u], in_=words[:, u, :], identity=identity[:])
 
-        for c in range(PASSES):
-            turn_h2(h2_rows[0], c, slice(0, F_HALF), nc.vector.tensor_copy)
-        x0_psum = fixed.tile([P, ROWS, F_X, PACK], BF16)
-        for c in range(PASSES):
-            nc.tensor.matmul(
-                out=x0_psum[:, c * F_TILE : (c + 1) * F_TILE].rearrange("p r g j -> p (r g j)"),
-                lhsT=identity_bf[:],
-                rhs=x0_tok[:, c].rearrange("p g j -> p (g j)").unsqueeze(1).to_broadcast([P, F_TILE, F_X * PACK]),
-                start=True,
-                stop=True,
-            )
+        h2_early = psum.tile([P, F_H, 2], F32, tag="bank")
+        turn_h2(0, h2_early)
+        h2_psum = fixed.tile([P, PASSES, F_H, 2], F32)
+        h2_tok = keep.tile([P, PASSES, F_H, PACK], BF16)
+
+        def copy_h2(c):
+            turned = psum.tile([P, F_H, 2], F32, tag="bank")
+            turn_h2(c, turned)
+            nc.scalar.copy(out=h2_tok[:, c].bitcast(F32), in_=turned[:])
+
+        copy_h2(0)
 
         pieces = cut_into_pieces()
         z_tiles = {}
+        out_rows = out.rearrange("(f g) n -> f g n", g=F_X)
 
-        def product(index):
+        def allocate(index):
             first, width, helped = pieces[index]
-            z = products.tile([P, width, ROWS, F_X, PACK], BF16, name="z", align_bytes=64)
+            z = products.tile([P, width, PASSES, F_H, PACK], BF16, name="z", align_bytes=64)
             z_tiles[index] = z
+
+        def product_of_pass(index, c, h2_c):
+            first, width, helped = pieces[index]
+            z = z_tiles[index]
             own = width - helped
-            shape = [P, own, ROWS, F_X, PACK]
+            shape = [P, own, F_H, PACK]
             nc.vector.tensor_tensor(
-                out=z[:, 0:own],
-                in0=h2_tok[:, first : first + own].unsqueeze(3).to_broadcast(shape),
-                in1=x0_psum[:].unsqueeze(1).to_broadcast(shape),
+                out=z[:, 0:own, c],
+                in0=x0_tok[:, first : first + own, c].unsqueeze(2).to_broadcast(shape),
+                in1=h2_c.unsqueeze(1).to_broadcast(shape),
                 op=ALU.mult,
             )
-            shape = [P, PASSES, F_TILE, F_X, PACK]
             for i in range(own, width):
                 nc.gpsimd.tensor_tensor(
-                    out=z[:, i].rearrange("p (c r) g j -> p c r g j", r=F_TILE),
-                    in0=h2_tok[:, first + i].rearrange("p (c r) j -> p c r j", r=F_TILE).unsqueeze(3).to_broadcast(shape),
-                    in1=x0_tok[:].unsqueeze(2).to_broadcast(shape),
+                    out=z[:, i, c],
+                    in0=x0_tok[:, first + i, c].unsqueeze(1).to_broadcast([P, F_H, PACK]),
+                    in1=h2_tok[:, c],
+                    op=ALU.mult,
+                )
+
+        def product(index):
+            allocate(index)
+            first, width, helped = pieces[index]
+            z = z_tiles[index]
+            own = width - helped
+            shape = [P, own, PASSES, F_H, PACK]
+            nc.vector.tensor_tensor(
+                out=z[:, 0:own],
+                in0=x0_tok[:, first : first + own].unsqueeze(3).to_broadcast(shape),
+                in1=h2_psum[:].bitcast(BF16).unsqueeze(1).to_broadcast(shape),
+                op=ALU.mult,
+            )
+            for i in range(own, width):
+                nc.gpsimd.tensor_tensor(
+                    out=z[:, i],
+                    in0=x0_tok[:, first + i].unsqueeze(2).to_broadcast([P, PASSES, F_H, PACK]),
+                    in1=h2_tok[:],
                     op=ALU.mult,
                 )
 
@@ -170,7 +183,7 @@ def tile_cin_pb_v_kernel(tc, h2, x0, W3, b3, pre, grad_out, out):
             nc.vector.quantize_mx(
                 out=z_codes[:].rearrange("p i c m -> p (i c m)").bitcast(E4M3X4),
                 scales=z_scales[:].rearrange("p i c m -> p (i c m)"),
-                in_=z_tiles[index][:, start : start + width].rearrange("p i q g j -> p (i q g j)"),
+                in_=z_tiles[index][:, start : start + width].rearrange("p i c f j -> p (i c f j)"),
             )
             sums = []
             for i in range(width):
@@ -193,11 +206,13 @@ def tile_cin_pb_v_kernel(tc, h2, x0, W3, b3, pre, grad_out, out):
             result = results.tile([P, width, N], F32)
             for i in range(width):
                 copy(out=result[:, i, :], in_=sums[i][:])
-            rows = out[first * P : (first + width) * P, :]
-            nc.sync.dma_start(out=rows.rearrange("(i m) n -> m i n", m=P), in_=result[:])
+            nc.sync.dma_start(out=out_rows[:, first : first + width, :], in_=result[:])
 
-        for index in range(HEAD):
-            product(index)
+        for index in range(EARLY):
+            allocate(index)
+            product_of_pass(index, 0, h2_early[:].bitcast(BF16))
+        for c in range(PASSES):
+            turn_h2(c, h2_psum[:, c])
 
         dp_codes = keep.tile([P, PASSES, N], U32, align_bytes=64)
         dp_scales = keep.tile([P, PASSES, N], U8, align_bytes=64)
@@ -206,9 +221,15 @@ def tile_cin_pb_v_kernel(tc, h2, x0, W3, b3, pre, grad_out, out):
         for c in range(PASSES):
             sign = keep.tile([P, N, PACK], BF16, name="sign%d" % c)
             nc.scalar.activation(out=sign[:], in_=pre_sb[c][:].rearrange("p j n -> p n j"), func=ACT.Sign)
+            if c == 0:
+                copy_h2(1)
             mask = keep.tile([P, N, PACK], BF16, name="mask%d" % c)
             nc.scalar.activation(out=mask[:], in_=sign[:], func=ACT.Relu)
             mask_of.append(mask)
+        for index in range(EARLY):
+            product_of_pass(index, 1, h2_psum[:, 1].bitcast(BF16))
+        for index in range(EARLY, HEAD):
+            product(index)
         for c in range(PASSES):
             for first in range(0, N, N_BANK):
                 grad_tok = psum.tile([P, N_BANK, PACK], BF16, tag="bank")
@@ -228,8 +249,6 @@ def tile_cin_pb_v_kernel(tc, h2, x0, W3, b3, pre, grad_out, out):
                     in1=grad_tok[:],
                     op=ALU.mult,
                 )
-        for c in range(PASSES):
-            turn_h2(h2_rows[1], c, slice(F_HALF, F_H), nc.scalar.copy)
         nc.vector.quantize_mx(
             out=dp_codes[:].rearrange("p c n -> p (c n)").bitcast(E5M2X4),
             scales=dp_scales[:].rearrange("p c n -> p (c n)"),

@@ -21,6 +21,8 @@ TOKENS = B_PASS * D
 TILES = F_X
 WIDEST = 4
 FULL = 2 * WIDEST
+STEADY = 8
+BUFFERS = 3
 HEAD = 3
 EARLY = 2
 N_BANK = 256
@@ -32,16 +34,16 @@ BYTES = 2 * (B * F_H * D + B * F_X * D + B * N) + 4 * B * D * N + 4 * F_H * F_X 
 
 
 def cut_into_pieces():
-    widths = [FULL] * (TILES // FULL - 1) + [2, 2, 1, 1, 1, 1]
+    widths = [FULL] * HEAD + [WIDEST] * STEADY + [2, 2, 1, 1, 1, 1]
     pieces = []
     first = 0
     for index, width in enumerate(widths):
-        if index == 0:
-            helped = 2
-        elif index == HEAD or index > TILES // FULL - 1:
-            helped = 0
-        else:
+        if index < HEAD:
+            helped = 4 if index == 0 else 2
+        elif width == WIDEST and not HEAD < index < HEAD + BUFFERS:
             helped = 1
+        else:
+            helped = 0
         pieces.append((first, width, helped))
         first += width
     assert first == TILES
@@ -52,7 +54,8 @@ def tile_cin_pb_v_kernel(tc, h2, x0, W3, b3, pre, grad_out, out):
     nc = tc.nc
     with ExitStack() as ctx:
         keep = ctx.enter_context(tc.tile_pool(name="keep", bufs=1))
-        products = ctx.enter_context(tc.tile_pool(name="products", bufs=3))
+        head_products = ctx.enter_context(tc.tile_pool(name="head_products", bufs=HEAD))
+        products = ctx.enter_context(tc.tile_pool(name="products", bufs=BUFFERS))
         quantised = ctx.enter_context(tc.tile_pool(name="quantised", bufs=6))
         results = ctx.enter_context(tc.tile_pool(name="results", bufs=8))
         psum = ctx.enter_context(tc.psum_pool(name="psum", bufs=7))
@@ -135,33 +138,31 @@ def tile_cin_pb_v_kernel(tc, h2, x0, W3, b3, pre, grad_out, out):
 
         def allocate(index):
             first, width, helped = pieces[index]
-            z = products.tile([P, width, PASSES, F_H, PACK], BF16, name="z", align_bytes=64)
+            pool = head_products if index < HEAD else products
+            z = pool.tile([P, width, PASSES, F_H, PACK], BF16, name="z", align_bytes=64)
             z_tiles[index] = z
+            units = [(i, c) for i in range(width) for c in range(PASSES)]
+            return first, z, units[len(units) - helped :], width - (helped + 1) // PASSES
 
-        def product_of_pass(index, c, h2_c):
-            first, width, helped = pieces[index]
-            z = z_tiles[index]
-            own = width - helped
-            shape = [P, own, F_H, PACK]
+        def multiply_pass(first, z, tiles, c, h2_c):
+            shape = [P, tiles.stop - tiles.start, F_H, PACK]
             nc.vector.tensor_tensor(
-                out=z[:, 0:own, c],
-                in0=x0_tok[:, first : first + own, c].unsqueeze(2).to_broadcast(shape),
+                out=z[:, tiles, c],
+                in0=x0_tok[:, first + tiles.start : first + tiles.stop, c].unsqueeze(2).to_broadcast(shape),
                 in1=h2_c.unsqueeze(1).to_broadcast(shape),
                 op=ALU.mult,
             )
-            for i in range(own, width):
-                nc.gpsimd.tensor_tensor(
-                    out=z[:, i, c],
-                    in0=x0_tok[:, first + i, c].unsqueeze(1).to_broadcast([P, F_H, PACK]),
-                    in1=h2_tok[:, c],
-                    op=ALU.mult,
-                )
+
+        def help_pass(first, z, i, c):
+            nc.gpsimd.tensor_tensor(
+                out=z[:, i, c],
+                in0=x0_tok[:, first + i, c].unsqueeze(1).to_broadcast([P, F_H, PACK]),
+                in1=h2_tok[:, c],
+                op=ALU.mult,
+            )
 
         def product(index):
-            allocate(index)
-            first, width, helped = pieces[index]
-            z = z_tiles[index]
-            own = width - helped
+            first, z, helped, own = allocate(index)
             shape = [P, own, PASSES, F_H, PACK]
             nc.vector.tensor_tensor(
                 out=z[:, 0:own],
@@ -169,13 +170,10 @@ def tile_cin_pb_v_kernel(tc, h2, x0, W3, b3, pre, grad_out, out):
                 in1=h2_psum[:].bitcast(BF16).unsqueeze(1).to_broadcast(shape),
                 op=ALU.mult,
             )
-            for i in range(own, width):
-                nc.gpsimd.tensor_tensor(
-                    out=z[:, i],
-                    in0=x0_tok[:, first + i].unsqueeze(2).to_broadcast([P, PASSES, F_H, PACK]),
-                    in1=h2_tok[:],
-                    op=ALU.mult,
-                )
+            if len(helped) % PASSES == 1:
+                multiply_pass(first, z, slice(own, own + 1), 0, h2_psum[:, 0].bitcast(BF16))
+            for i, c in helped:
+                help_pass(first, z, i, c)
 
         def finish(index, start, width):
             z_codes = quantised.tile([P, width, PASSES, P], U32, align_bytes=64)
@@ -208,9 +206,12 @@ def tile_cin_pb_v_kernel(tc, h2, x0, W3, b3, pre, grad_out, out):
                 copy(out=result[:, i, :], in_=sums[i][:])
             nc.sync.dma_start(out=out_rows[:, first : first + width, :], in_=result[:])
 
-        for index in range(EARLY):
-            allocate(index)
-            product_of_pass(index, 0, h2_early[:].bitcast(BF16))
+        early = [allocate(index) for index in range(EARLY)]
+        for first, z, helped, own in early:
+            multiply_pass(first, z, slice(0, own), 0, h2_early[:].bitcast(BF16))
+            for i, c in helped:
+                if c == 0:
+                    help_pass(first, z, i, c)
         for c in range(PASSES):
             turn_h2(c, h2_psum[:, c])
 
@@ -226,8 +227,11 @@ def tile_cin_pb_v_kernel(tc, h2, x0, W3, b3, pre, grad_out, out):
             mask = keep.tile([P, N, PACK], BF16, name="mask%d" % c)
             nc.scalar.activation(out=mask[:], in_=sign[:], func=ACT.Relu)
             mask_of.append(mask)
-        for index in range(EARLY):
-            product_of_pass(index, 1, h2_psum[:, 1].bitcast(BF16))
+        for first, z, helped, own in early:
+            multiply_pass(first, z, slice(0, own), 1, h2_psum[:, 1].bitcast(BF16))
+            for i, c in helped:
+                if c == 1:
+                    help_pass(first, z, i, c)
         for index in range(EARLY, HEAD):
             product(index)
         for c in range(PASSES):
@@ -256,10 +260,9 @@ def tile_cin_pb_v_kernel(tc, h2, x0, W3, b3, pre, grad_out, out):
         )
 
         left = []
-        for index in range(len(pieces)):
+        for index, (first, width, helped) in enumerate(pieces):
             if HEAD - 1 <= index < len(pieces) - 1:
                 product(index + 1)
-            first, width, helped = pieces[index]
             for start in range(0, width, WIDEST):
                 sums = finish(index, start, min(WIDEST, width))
                 if index < len(pieces) - LAST:

@@ -24,7 +24,7 @@ FULL = 2 * WIDEST
 STEADY = 8
 BUFFERS = 3
 HEAD = 3
-EARLY = 2
+X_EARLY = 32
 N_BANK = 256
 N_PLAIN = 128
 LAST = 3
@@ -62,12 +62,13 @@ def tile_cin_pb_v_kernel(tc, h2, x0, W3, b3, pre, grad_out, out):
         fixed = ctx.enter_context(tc.psum_pool(name="fixed", bufs=1))
         ctx.enter_context(tc.manual_schedule())
 
-        x0_rows = keep.tile([P, TOKENS], BF16)
-        for c, queue in enumerate((nc.sync, nc.scalar)):
-            queue.dma_start(
-                out=x0_rows[c * F_X : (c + 1) * F_X, :].rearrange("g (b d) -> g b d", d=D),
-                in_=x0[c * B_PASS : (c + 1) * B_PASS].rearrange("b g d -> g b d"),
-            )
+        x0_early_rows = keep.tile([P, TOKENS], BF16)
+        nc.sync.dma_start(
+            out=x0_early_rows[0:X_EARLY, :].rearrange("g (b d) -> g b d", d=D),
+            in_=x0[0:B_PASS, 0:X_EARLY, :].rearrange("b g d -> g b d"),
+        )
+        nc.vector.memset(x0_early_rows[X_EARLY : 2 * X_EARLY, :], 0.0)
+        nc.vector.memset(x0_early_rows[2 * X_EARLY : P, :], 0.0)
         h2_rows = []
         for c in range(PASSES):
             rows = keep.tile([P, TOKENS], BF16, name="h2_rows%d" % c)
@@ -79,20 +80,29 @@ def tile_cin_pb_v_kernel(tc, h2, x0, W3, b3, pre, grad_out, out):
                 in_=h2[c * B_PASS : (c + 1) * B_PASS, fields, :].rearrange("b f d -> f b d"),
             )
 
-        load_h2(nc.sync, 0, slice(0, F_H // 2))
-        load_h2(nc.scalar, 0, slice(F_H // 2, F_H))
+        load_h2(nc.scalar, 0, slice(0, F_H // 2))
+        load_h2(nc.sync, 0, slice(F_H // 2, F_H))
+        pre_rows = pre.rearrange("b d n -> (b d) n").rearrange("(c p j) n -> c p j n", c=PASSES, j=PACK)
+        pre_sb = []
+
+        def load_pre(c):
+            pre_c = keep.tile([P, PACK, N], F32, name="pre_sb%d" % c)
+            nc.scalar.dma_start(out=pre_c[:], in_=pre_rows[c])
+            pre_sb.append(pre_c)
+
+        load_pre(0)
+        x0_rows = keep.tile([P, TOKENS], BF16)
+        for c in range(PASSES):
+            nc.scalar.dma_start(
+                out=x0_rows[c * F_X : (c + 1) * F_X, :].rearrange("g (b d) -> g b d", d=D),
+                in_=x0[c * B_PASS : (c + 1) * B_PASS].rearrange("b g d -> g b d"),
+            )
+        load_h2(nc.scalar, 1, slice(0, F_H))
         grad_rows = keep.tile([P, N], BF16)
         nc.scalar.dma_start(out=grad_rows[0:B, :], in_=grad_out)
         nc.vector.memset(grad_rows[B : 2 * B, :], 0.0)
         nc.vector.memset(grad_rows[2 * B : P, :], 0.0)
-        pre_rows = pre.rearrange("b d n -> (b d) n").rearrange("(c p j) n -> c p j n", c=PASSES, j=PACK)
-        pre_sb = []
-        for c in range(PASSES):
-            pre_c = keep.tile([P, PACK, N], F32, name="pre_sb%d" % c)
-            nc.scalar.dma_start(out=pre_c[:], in_=pre_rows[c])
-            pre_sb.append(pre_c)
-            if c == 0:
-                load_h2(nc.scalar, 1, slice(0, F_H))
+        load_pre(1)
 
         warm = keep.tile([P, 2], F32)
         nc.vector.memset(warm[:], 0.0)
@@ -106,13 +116,17 @@ def tile_cin_pb_v_kernel(tc, h2, x0, W3, b3, pre, grad_out, out):
         )
         spread_cols = spread[:].rearrange("k b r -> k (b r)")
 
-        x0_words = x0_rows[:].bitcast(F32).rearrange("q (p u) -> q u p", u=2)
-        x0_turned = psum.tile([P, 2, P], F32, tag="bank")
-        for u in range(2):
-            nc.tensor.transpose(out=x0_turned[:, u, :], in_=x0_words[:, u, :], identity=identity[:])
-        x0_tok = keep.tile([P, F_X, PASSES, PACK], BF16)
+        def turn_x0(rows):
+            words = rows[:].bitcast(F32).rearrange("q (p u) -> q u p", u=2)
+            turned = psum.tile([P, 2, P], F32, tag="bank")
+            for u in range(2):
+                nc.tensor.transpose(out=turned[:, u, :], in_=words[:, u, :], identity=identity[:])
+            return turned
+
+        x0_early_turned = turn_x0(x0_early_rows)
+        x0_early = keep.tile([P, X_EARLY, PACK], BF16)
         nc.vector.tensor_copy(
-            out=x0_tok[:].bitcast(F32), in_=x0_turned[:].rearrange("p u (c g) -> p g c u", c=PASSES)
+            out=x0_early[:].bitcast(F32), in_=x0_early_turned[:, :, 0:X_EARLY].rearrange("p u g -> p g u")
         )
 
         def turn_h2(c, turned):
@@ -144,19 +158,19 @@ def tile_cin_pb_v_kernel(tc, h2, x0, W3, b3, pre, grad_out, out):
             units = [(i, c) for i in range(width) for c in range(PASSES)]
             return first, z, units[len(units) - helped :], width - (helped + 1) // PASSES
 
-        def multiply_pass(first, z, tiles, c, h2_c):
+        def multiply_pass(z, tiles, c, x0_c, h2_c):
             shape = [P, tiles.stop - tiles.start, F_H, PACK]
             nc.vector.tensor_tensor(
                 out=z[:, tiles, c],
-                in0=x0_tok[:, first + tiles.start : first + tiles.stop, c].unsqueeze(2).to_broadcast(shape),
+                in0=x0_c.unsqueeze(2).to_broadcast(shape),
                 in1=h2_c.unsqueeze(1).to_broadcast(shape),
                 op=ALU.mult,
             )
 
-        def help_pass(first, z, i, c):
+        def help_pass(z, i, c, x0_c):
             nc.gpsimd.tensor_tensor(
                 out=z[:, i, c],
-                in0=x0_tok[:, first + i, c].unsqueeze(1).to_broadcast([P, F_H, PACK]),
+                in0=x0_c.unsqueeze(1).to_broadcast([P, F_H, PACK]),
                 in1=h2_tok[:, c],
                 op=ALU.mult,
             )
@@ -171,9 +185,10 @@ def tile_cin_pb_v_kernel(tc, h2, x0, W3, b3, pre, grad_out, out):
                 op=ALU.mult,
             )
             if len(helped) % PASSES == 1:
-                multiply_pass(first, z, slice(own, own + 1), 0, h2_psum[:, 0].bitcast(BF16))
+                tiles = slice(own, own + 1)
+                multiply_pass(z, tiles, 0, x0_tok[:, first + own : first + own + 1, 0], h2_psum[:, 0].bitcast(BF16))
             for i, c in helped:
-                help_pass(first, z, i, c)
+                help_pass(z, i, c, x0_tok[:, first + i, c])
 
         def finish(index, start, width):
             z_codes = quantised.tile([P, width, PASSES, P], U32, align_bytes=64)
@@ -206,12 +221,17 @@ def tile_cin_pb_v_kernel(tc, h2, x0, W3, b3, pre, grad_out, out):
                 copy(out=result[:, i, :], in_=sums[i][:])
             nc.sync.dma_start(out=out_rows[:, first : first + width, :], in_=result[:])
 
-        early = [allocate(index) for index in range(EARLY)]
-        for first, z, helped, own in early:
-            multiply_pass(first, z, slice(0, own), 0, h2_early[:].bitcast(BF16))
+        head = [allocate(index) for index in range(HEAD)]
+        for first, z, helped, own in head:
+            multiply_pass(z, slice(0, own), 0, x0_early[:, first : first + own], h2_early[:].bitcast(BF16))
             for i, c in helped:
                 if c == 0:
-                    help_pass(first, z, i, c)
+                    help_pass(z, i, c, x0_early[:, first + i])
+        x0_turned = turn_x0(x0_rows)
+        x0_tok = keep.tile([P, F_X, PASSES, PACK], BF16)
+        nc.vector.tensor_copy(
+            out=x0_tok[:].bitcast(F32), in_=x0_turned[:].rearrange("p u (c g) -> p g c u", c=PASSES)
+        )
         for c in range(PASSES):
             turn_h2(c, h2_psum[:, c])
 
@@ -227,13 +247,12 @@ def tile_cin_pb_v_kernel(tc, h2, x0, W3, b3, pre, grad_out, out):
             mask = keep.tile([P, N, PACK], BF16, name="mask%d" % c)
             nc.scalar.activation(out=mask[:], in_=sign[:], func=ACT.Relu)
             mask_of.append(mask)
-        for first, z, helped, own in early:
-            multiply_pass(first, z, slice(0, own), 1, h2_psum[:, 1].bitcast(BF16))
+        for first, z, helped, own in head:
+            multiply_pass(z, slice(0, own), 1, x0_tok[:, first : first + own, 1], h2_psum[:, 1].bitcast(BF16))
             for i, c in helped:
                 if c == 1:
-                    help_pass(first, z, i, c)
-        for index in range(EARLY, HEAD):
-            product(index)
+                    help_pass(z, i, c, x0_tok[:, first + i, c])
+        product(HEAD)
         for c in range(PASSES):
             for first in range(0, N, N_BANK):
                 grad_tok = psum.tile([P, N_BANK, PACK], BF16, tag="bank")
@@ -261,7 +280,7 @@ def tile_cin_pb_v_kernel(tc, h2, x0, W3, b3, pre, grad_out, out):
 
         left = []
         for index, (first, width, helped) in enumerate(pieces):
-            if HEAD - 1 <= index < len(pieces) - 1:
+            if HEAD <= index < len(pieces) - 1:
                 product(index + 1)
             for start in range(0, width, WIDEST):
                 sums = finish(index, start, min(WIDEST, width))

@@ -63,12 +63,18 @@ def tile_cin_pb_v_kernel(tc, h2, x0, W3, b3, pre, grad_out, out):
         ctx.enter_context(tc.manual_schedule())
 
         x0_early_rows = keep.tile([P, TOKENS], BF16)
-        nc.sync.dma_start(
-            out=x0_early_rows[0:X_EARLY, :].rearrange("g (b d) -> g b d", d=D),
-            in_=x0[0:B_PASS, 0:X_EARLY, :].rearrange("b g d -> g b d"),
-        )
+        x0_late_rows = keep.tile([P, TOKENS], BF16)
+
+        def load_x0(rows, c, fields):
+            nc.sync.dma_start(
+                out=rows[c * F_X + fields.start : c * F_X + fields.stop, :].rearrange("g (b d) -> g b d", d=D),
+                in_=x0[c * B_PASS : (c + 1) * B_PASS, fields].rearrange("b g d -> g b d"),
+            )
+
+        load_x0(x0_early_rows, 0, slice(0, X_EARLY))
         nc.vector.memset(x0_early_rows[X_EARLY : 2 * X_EARLY, :], 0.0)
         nc.vector.memset(x0_early_rows[2 * X_EARLY : P, :], 0.0)
+        nc.vector.memset(x0_late_rows[0:X_EARLY, :], 0.0)
         h2_rows = []
         for c in range(PASSES):
             rows = keep.tile([P, TOKENS], BF16, name="h2_rows%d" % c)
@@ -87,19 +93,15 @@ def tile_cin_pb_v_kernel(tc, h2, x0, W3, b3, pre, grad_out, out):
 
         def load_pre(c):
             pre_c = keep.tile([P, PACK, N], F32, name="pre_sb%d" % c)
-            nc.scalar.dma_start(out=pre_c[:], in_=pre_rows[c])
+            nc.sync.dma_start(out=pre_c[:], in_=pre_rows[c])
             pre_sb.append(pre_c)
 
         load_pre(0)
-        x0_rows = keep.tile([P, TOKENS], BF16)
-        for c in range(PASSES):
-            nc.scalar.dma_start(
-                out=x0_rows[c * F_X : (c + 1) * F_X, :].rearrange("g (b d) -> g b d", d=D),
-                in_=x0[c * B_PASS : (c + 1) * B_PASS].rearrange("b g d -> g b d"),
-            )
-        load_h2(nc.scalar, 1, slice(0, F_H))
+        load_x0(x0_late_rows, 0, slice(X_EARLY, F_X))
+        load_x0(x0_late_rows, 1, slice(0, F_X))
+        load_h2(nc.sync, 1, slice(0, F_H))
         grad_rows = keep.tile([P, N], BF16)
-        nc.scalar.dma_start(out=grad_rows[0:B, :], in_=grad_out)
+        nc.sync.dma_start(out=grad_rows[0:B, :], in_=grad_out)
         nc.vector.memset(grad_rows[B : 2 * B, :], 0.0)
         nc.vector.memset(grad_rows[2 * B : P, :], 0.0)
         load_pre(1)
@@ -118,16 +120,21 @@ def tile_cin_pb_v_kernel(tc, h2, x0, W3, b3, pre, grad_out, out):
 
         def turn_x0(rows):
             words = rows[:].bitcast(F32).rearrange("q (p u) -> q u p", u=2)
-            turned = psum.tile([P, 2, P], F32, tag="bank")
+            turned = psum.tile([P, 2, PASSES, F_X], F32, tag="bank")
             for u in range(2):
-                nc.tensor.transpose(out=turned[:, u, :], in_=words[:, u, :], identity=identity[:])
+                nc.tensor.transpose(
+                    out=turned[:, u].rearrange("p c g -> p (c g)"), in_=words[:, u, :], identity=identity[:]
+                )
             return turned
 
-        x0_early_turned = turn_x0(x0_early_rows)
-        x0_early = keep.tile([P, X_EARLY, PACK], BF16)
-        nc.vector.tensor_copy(
-            out=x0_early[:].bitcast(F32), in_=x0_early_turned[:, :, 0:X_EARLY].rearrange("p u g -> p g u")
-        )
+        x0_tok = keep.tile([P, F_X, PASSES, PACK], BF16)
+
+        def copy_x0(turned, c, fields):
+            nc.vector.tensor_copy(
+                out=x0_tok[:].bitcast(F32)[:, fields, c], in_=turned[:, :, c, fields].rearrange("p u g -> p g u")
+            )
+
+        copy_x0(turn_x0(x0_early_rows), 0, slice(0, X_EARLY))
 
         def turn_h2(c, turned):
             words = h2_rows[c][:].bitcast(F32).rearrange("f (p u) -> f u p", u=2)
@@ -139,12 +146,12 @@ def tile_cin_pb_v_kernel(tc, h2, x0, W3, b3, pre, grad_out, out):
         h2_psum = fixed.tile([P, PASSES, F_H, 2], F32)
         h2_tok = keep.tile([P, PASSES, F_H, PACK], BF16)
 
-        def copy_h2(c):
+        def copy_h2(c, copy):
             turned = psum.tile([P, F_H, 2], F32, tag="bank")
             turn_h2(c, turned)
-            nc.scalar.copy(out=h2_tok[:, c].bitcast(F32), in_=turned[:])
+            copy(out=h2_tok[:, c].bitcast(F32), in_=turned[:])
 
-        copy_h2(0)
+        copy_h2(0, nc.scalar.copy)
 
         pieces = cut_into_pieces()
         z_tiles = {}
@@ -223,17 +230,15 @@ def tile_cin_pb_v_kernel(tc, h2, x0, W3, b3, pre, grad_out, out):
 
         head = [allocate(index) for index in range(HEAD)]
         for first, z, helped, own in head:
-            multiply_pass(z, slice(0, own), 0, x0_early[:, first : first + own], h2_early[:].bitcast(BF16))
+            multiply_pass(z, slice(0, own), 0, x0_tok[:, first : first + own, 0], h2_early[:].bitcast(BF16))
             for i, c in helped:
                 if c == 0:
-                    help_pass(z, i, c, x0_early[:, first + i])
-        x0_turned = turn_x0(x0_rows)
-        x0_tok = keep.tile([P, F_X, PASSES, PACK], BF16)
-        nc.vector.tensor_copy(
-            out=x0_tok[:].bitcast(F32), in_=x0_turned[:].rearrange("p u (c g) -> p g c u", c=PASSES)
-        )
-        for c in range(PASSES):
-            turn_h2(c, h2_psum[:, c])
+                    help_pass(z, i, c, x0_tok[:, first + i, c])
+        x0_late_turned = turn_x0(x0_late_rows)
+        copy_x0(x0_late_turned, 1, slice(0, F_X))
+        turn_h2(0, h2_psum[:, 0])
+        copy_h2(1, nc.vector.tensor_copy)
+        turn_h2(1, h2_psum[:, 1])
 
         dp_codes = keep.tile([P, PASSES, N], U32, align_bytes=64)
         dp_scales = keep.tile([P, PASSES, N], U8, align_bytes=64)
@@ -242,8 +247,6 @@ def tile_cin_pb_v_kernel(tc, h2, x0, W3, b3, pre, grad_out, out):
         for c in range(PASSES):
             sign = keep.tile([P, N, PACK], BF16, name="sign%d" % c)
             nc.scalar.activation(out=sign[:], in_=pre_sb[c][:].rearrange("p j n -> p n j"), func=ACT.Sign)
-            if c == 0:
-                copy_h2(1)
             mask = keep.tile([P, N, PACK], BF16, name="mask%d" % c)
             nc.scalar.activation(out=mask[:], in_=sign[:], func=ACT.Relu)
             mask_of.append(mask)
@@ -252,7 +255,7 @@ def tile_cin_pb_v_kernel(tc, h2, x0, W3, b3, pre, grad_out, out):
             for i, c in helped:
                 if c == 1:
                     help_pass(z, i, c, x0_tok[:, first + i, c])
-        product(HEAD)
+        copy_x0(x0_late_turned, 0, slice(X_EARLY, F_X))
         for c in range(PASSES):
             for first in range(0, N, N_BANK):
                 grad_tok = psum.tile([P, N_BANK, PACK], BF16, tag="bank")
@@ -280,7 +283,7 @@ def tile_cin_pb_v_kernel(tc, h2, x0, W3, b3, pre, grad_out, out):
 
         left = []
         for index, (first, width, helped) in enumerate(pieces):
-            if HEAD <= index < len(pieces) - 1:
+            if HEAD - 1 <= index < len(pieces) - 1:
                 product(index + 1)
             for start in range(0, width, WIDEST):
                 sums = finish(index, start, min(WIDEST, width))

@@ -20,11 +20,12 @@ B_PASS = B // PASSES
 TOKENS = B_PASS * D
 TILES = F_X
 WIDEST = 4
-FULL = 2 * WIDEST
-STEADY = 8
-BUFFERS = 3
-HEAD = 3
+HEAD = 24
+HEAD_SHARE = 20
 X_EARLY = 32
+STEADY = 8
+SHARE = 16
+BUFFERS = 3
 N_BANK = 256
 N_PLAIN = 128
 LAST = 3
@@ -34,17 +35,11 @@ BYTES = 2 * (B * F_H * D + B * F_X * D + B * N) + 4 * B * D * N + 4 * F_H * F_X 
 
 
 def cut_into_pieces():
-    widths = [FULL] * HEAD + [WIDEST] * STEADY + [2, 2, 1, 1, 1, 1]
+    widths = [WIDEST] * STEADY + [2, 2, 1, 1, 1, 1]
     pieces = []
-    first = 0
+    first = HEAD
     for index, width in enumerate(widths):
-        if index < HEAD:
-            helped = 4 if index == 0 else 2
-        elif width == WIDEST and not HEAD < index < HEAD + BUFFERS:
-            helped = 1
-        else:
-            helped = 0
-        pieces.append((first, width, helped))
+        pieces.append((first, width, SHARE if width > 1 and not 0 < index < BUFFERS else 0))
         first += width
     assert first == TILES
     return pieces
@@ -54,7 +49,6 @@ def tile_cin_pb_v_kernel(tc, h2, x0, W3, b3, pre, grad_out, out):
     nc = tc.nc
     with ExitStack() as ctx:
         keep = ctx.enter_context(tc.tile_pool(name="keep", bufs=1))
-        head_products = ctx.enter_context(tc.tile_pool(name="head_products", bufs=HEAD))
         products = ctx.enter_context(tc.tile_pool(name="products", bufs=BUFFERS))
         quantised = ctx.enter_context(tc.tile_pool(name="quantised", bufs=6))
         results = ctx.enter_context(tc.tile_pool(name="results", bufs=8))
@@ -129,12 +123,12 @@ def tile_cin_pb_v_kernel(tc, h2, x0, W3, b3, pre, grad_out, out):
 
         x0_tok = keep.tile([P, F_X, PASSES, PACK], BF16)
 
-        def copy_x0(turned, c, fields):
-            nc.vector.tensor_copy(
+        def copy_x0(turned, c, fields, copy):
+            copy(
                 out=x0_tok[:].bitcast(F32)[:, fields, c], in_=turned[:, :, c, fields].rearrange("p u g -> p g u")
             )
 
-        copy_x0(turn_x0(x0_early_rows), 0, slice(0, X_EARLY))
+        copy_x0(turn_x0(x0_early_rows), 0, slice(0, X_EARLY), nc.vector.tensor_copy)
 
         def turn_h2(c, turned):
             words = h2_rows[c][:].bitcast(F32).rearrange("f (p u) -> f u p", u=2)
@@ -157,53 +151,46 @@ def tile_cin_pb_v_kernel(tc, h2, x0, W3, b3, pre, grad_out, out):
         z_tiles = {}
         out_rows = out.rearrange("(f g) n -> f g n", g=F_X)
 
-        def allocate(index):
-            first, width, helped = pieces[index]
-            pool = head_products if index < HEAD else products
-            z = pool.tile([P, width, PASSES, F_H, PACK], BF16, name="z", align_bytes=64)
-            z_tiles[index] = z
-            units = [(i, c) for i in range(width) for c in range(PASSES)]
-            return first, z, units[len(units) - helped :], width - (helped + 1) // PASSES
-
-        def multiply_pass(z, tiles, c, x0_c, h2_c):
-            shape = [P, tiles.stop - tiles.start, F_H, PACK]
-            nc.vector.tensor_tensor(
-                out=z[:, tiles, c],
-                in0=x0_c.unsqueeze(2).to_broadcast(shape),
-                in1=h2_c.unsqueeze(1).to_broadcast(shape),
-                op=ALU.mult,
-            )
-
-        def help_pass(z, i, c, x0_c):
-            nc.gpsimd.tensor_tensor(
-                out=z[:, i, c],
-                in0=x0_c.unsqueeze(1).to_broadcast([P, F_H, PACK]),
-                in1=h2_tok[:, c],
-                op=ALU.mult,
-            )
+        def multiply_pass(z, first, c, share, h2_c):
+            width = z.shape[1]
+            x0_c = x0_tok[:, first : first + width, c].unsqueeze(2)
+            for engine, fields, h2_part in (
+                (nc.vector, slice(0, F_H - share), h2_c),
+                (nc.gpsimd, slice(F_H - share, F_H), h2_tok[:, c]),
+            ):
+                shape = [P, width, fields.stop - fields.start, PACK]
+                engine.tensor_tensor(
+                    out=z[:, :, c, fields],
+                    in0=x0_c.to_broadcast(shape),
+                    in1=h2_part[:, fields].unsqueeze(1).to_broadcast(shape),
+                    op=ALU.mult,
+                )
 
         def product(index):
-            first, z, helped, own = allocate(index)
-            shape = [P, own, PASSES, F_H, PACK]
-            nc.vector.tensor_tensor(
-                out=z[:, 0:own],
-                in0=x0_tok[:, first : first + own].unsqueeze(3).to_broadcast(shape),
-                in1=h2_psum[:].bitcast(BF16).unsqueeze(1).to_broadcast(shape),
-                op=ALU.mult,
-            )
-            if len(helped) % PASSES == 1:
-                tiles = slice(own, own + 1)
-                multiply_pass(z, tiles, 0, x0_tok[:, first + own : first + own + 1, 0], h2_psum[:, 0].bitcast(BF16))
-            for i, c in helped:
-                help_pass(z, i, c, x0_tok[:, first + i, c])
+            first, width, share = pieces[index]
+            z = products.tile([P, width, PASSES, F_H, PACK], BF16, name="z", align_bytes=64)
+            z_tiles[index] = z
+            x0_both = x0_tok[:, first : first + width].unsqueeze(3)
+            for engine, fields, h2_both in (
+                (nc.vector, slice(0, F_H - share), h2_psum[:].bitcast(BF16)),
+                (nc.gpsimd, slice(F_H - share, F_H), h2_tok[:]),
+            ):
+                shape = [P, width, PASSES, fields.stop - fields.start, PACK]
+                if fields.start < fields.stop:
+                    engine.tensor_tensor(
+                        out=z[:, :, :, fields],
+                        in0=x0_both.to_broadcast(shape),
+                        in1=h2_both[:, :, fields].unsqueeze(1).to_broadcast(shape),
+                        op=ALU.mult,
+                    )
 
-        def finish(index, start, width):
+        def finish(z, start, width):
             z_codes = quantised.tile([P, width, PASSES, P], U32, align_bytes=64)
             z_scales = quantised.tile([P, width, PASSES, P], U8, align_bytes=64)
             nc.vector.quantize_mx(
                 out=z_codes[:].rearrange("p i c m -> p (i c m)").bitcast(E4M3X4),
                 scales=z_scales[:].rearrange("p i c m -> p (i c m)"),
-                in_=z_tiles[index][:, start : start + width].rearrange("p i c f j -> p (i c f j)"),
+                in_=z[:, start : start + width].rearrange("p i c f j -> p (i c f j)"),
             )
             sums = []
             for i in range(width):
@@ -228,14 +215,10 @@ def tile_cin_pb_v_kernel(tc, h2, x0, W3, b3, pre, grad_out, out):
                 copy(out=result[:, i, :], in_=sums[i][:])
             nc.sync.dma_start(out=out_rows[:, first : first + width, :], in_=result[:])
 
-        head = [allocate(index) for index in range(HEAD)]
-        for first, z, helped, own in head:
-            multiply_pass(z, slice(0, own), 0, x0_tok[:, first : first + own, 0], h2_early[:].bitcast(BF16))
-            for i, c in helped:
-                if c == 0:
-                    help_pass(z, i, c, x0_tok[:, first + i, c])
+        z_head = keep.tile([P, HEAD, PASSES, F_H, PACK], BF16, align_bytes=64)
+        multiply_pass(z_head, 0, 0, HEAD_SHARE, h2_early[:].bitcast(BF16))
         x0_late_turned = turn_x0(x0_late_rows)
-        copy_x0(x0_late_turned, 1, slice(0, F_X))
+        copy_x0(x0_late_turned, 1, slice(0, F_X), nc.vector.tensor_copy)
         turn_h2(0, h2_psum[:, 0])
         copy_h2(1, nc.vector.tensor_copy)
         turn_h2(1, h2_psum[:, 1])
@@ -250,12 +233,8 @@ def tile_cin_pb_v_kernel(tc, h2, x0, W3, b3, pre, grad_out, out):
             mask = keep.tile([P, N, PACK], BF16, name="mask%d" % c)
             nc.scalar.activation(out=mask[:], in_=sign[:], func=ACT.Relu)
             mask_of.append(mask)
-        for first, z, helped, own in head:
-            multiply_pass(z, slice(0, own), 1, x0_tok[:, first : first + own, 1], h2_psum[:, 1].bitcast(BF16))
-            for i, c in helped:
-                if c == 1:
-                    help_pass(z, i, c, x0_tok[:, first + i, c])
-        copy_x0(x0_late_turned, 0, slice(X_EARLY, F_X))
+        multiply_pass(z_head, 0, 1, HEAD_SHARE, h2_psum[:, 1].bitcast(BF16))
+        copy_x0(x0_late_turned, 0, slice(X_EARLY, F_X), nc.scalar.copy)
         for c in range(PASSES):
             for first in range(0, N, N_BANK):
                 grad_tok = psum.tile([P, N_BANK, PACK], BF16, tag="bank")
@@ -281,15 +260,18 @@ def tile_cin_pb_v_kernel(tc, h2, x0, W3, b3, pre, grad_out, out):
             in_=dp[:].rearrange("p c n j -> p (c n j)"),
         )
 
+        for start in range(0, HEAD, WIDEST):
+            if start == HEAD - 2 * WIDEST:
+                product(0)
+            store(start, finish(z_head, start, WIDEST), nc.scalar.copy)
         left = []
-        for index, (first, width, helped) in enumerate(pieces):
-            if HEAD - 1 <= index < len(pieces) - 1:
+        for index, (first, width, share) in enumerate(pieces):
+            if index < len(pieces) - 1:
                 product(index + 1)
-            for start in range(0, width, WIDEST):
-                sums = finish(index, start, min(WIDEST, width))
-                if index < len(pieces) - LAST:
-                    store(first + start, sums, nc.scalar.copy)
-                else:
-                    left.append((first + start, sums))
+            sums = finish(z_tiles[index], 0, width)
+            if index < len(pieces) - LAST:
+                store(first, sums, nc.scalar.copy)
+            else:
+                left.append((first, sums))
         for first, sums in left:
             store(first, sums, nc.vector.tensor_copy)

@@ -26,8 +26,10 @@ X_EARLY = 32
 STEADY = 8
 SHARE = 16
 BUFFERS = 3
+STORED = 2
 N_BANK = 256
 N_PLAIN = 128
+DIAG = 1
 LAST = 3
 
 FLOPS = 2 * B * D * F_H * F_X * N
@@ -50,7 +52,8 @@ def tile_cin_pb_v_kernel(tc, h2, x0, W3, b3, pre, grad_out, out):
     with ExitStack() as ctx:
         keep = ctx.enter_context(tc.tile_pool(name="keep", bufs=1))
         products = ctx.enter_context(tc.tile_pool(name="products", bufs=BUFFERS))
-        quantised = ctx.enter_context(tc.tile_pool(name="quantised", bufs=6))
+        quantised = ctx.enter_context(tc.tile_pool(name="quantised", bufs=8))
+        diagonals = ctx.enter_context(tc.tile_pool(name="diagonals", bufs=2))
         results = ctx.enter_context(tc.tile_pool(name="results", bufs=8))
         psum = ctx.enter_context(tc.psum_pool(name="psum", bufs=7))
         fixed = ctx.enter_context(tc.psum_pool(name="fixed", bufs=1))
@@ -151,40 +154,40 @@ def tile_cin_pb_v_kernel(tc, h2, x0, W3, b3, pre, grad_out, out):
         z_tiles = {}
         out_rows = out.rearrange("(f g) n -> f g n", g=F_X)
 
-        def multiply_pass(z, first, c, share, h2_c):
-            width = z.shape[1]
-            x0_c = x0_tok[:, first : first + width, c].unsqueeze(2)
-            for engine, fields, h2_part in (
-                (nc.vector, slice(0, F_H - share), h2_c),
-                (nc.gpsimd, slice(F_H - share, F_H), h2_tok[:, c]),
-            ):
-                shape = [P, width, fields.stop - fields.start, PACK]
-                engine.tensor_tensor(
-                    out=z[:, :, c, fields],
-                    in0=x0_c.to_broadcast(shape),
-                    in1=h2_part[:, fields].unsqueeze(1).to_broadcast(shape),
-                    op=ALU.mult,
-                )
+        def multiply_pass(engine, z, tiles, first, c, fields, h2_c):
+            shape = [P, tiles.stop - tiles.start, fields.stop - fields.start, PACK]
+            engine.tensor_tensor(
+                out=z[:, tiles, c, fields],
+                in0=x0_tok[:, first + tiles.start : first + tiles.stop, c].unsqueeze(2).to_broadcast(shape),
+                in1=h2_c[:, fields].unsqueeze(1).to_broadcast(shape),
+                op=ALU.mult,
+            )
 
-        def product(index):
+        def allocate(index):
             first, width, share = pieces[index]
             z = products.tile([P, width, PASSES, F_H, PACK], BF16, name="z", align_bytes=64)
             z_tiles[index] = z
-            x0_both = x0_tok[:, first : first + width].unsqueeze(3)
+
+        def product(index):
+            if index > 0:
+                allocate(index)
+            first, width, share = pieces[index]
+            own = width - DIAG if index == 0 else width
+            x0_both = x0_tok[:, first : first + own].unsqueeze(3)
             for engine, fields, h2_both in (
                 (nc.vector, slice(0, F_H - share), h2_psum[:].bitcast(BF16)),
                 (nc.gpsimd, slice(F_H - share, F_H), h2_tok[:]),
             ):
-                shape = [P, width, PASSES, fields.stop - fields.start, PACK]
+                shape = [P, own, PASSES, fields.stop - fields.start, PACK]
                 if fields.start < fields.stop:
                     engine.tensor_tensor(
-                        out=z[:, :, :, fields],
+                        out=z_tiles[index][:, 0:own, :, fields],
                         in0=x0_both.to_broadcast(shape),
                         in1=h2_both[:, :, fields].unsqueeze(1).to_broadcast(shape),
                         op=ALU.mult,
                     )
 
-        def finish(z, start, width):
+        def quantise(z, start, width):
             z_codes = quantised.tile([P, width, PASSES, P], U32, align_bytes=64)
             z_scales = quantised.tile([P, width, PASSES, P], U8, align_bytes=64)
             nc.vector.quantize_mx(
@@ -192,8 +195,11 @@ def tile_cin_pb_v_kernel(tc, h2, x0, W3, b3, pre, grad_out, out):
                 scales=z_scales[:].rearrange("p i c m -> p (i c m)"),
                 in_=z[:, start : start + width].rearrange("p i c f j -> p (i c f j)"),
             )
+            return z_codes, z_scales
+
+        def multiply(z_codes, z_scales):
             sums = []
-            for i in range(width):
+            for i in range(z_codes.shape[1]):
                 acc = psum.tile([P, N], F32, tag="bank")
                 sums.append(acc)
                 for c in range(PASSES):
@@ -216,7 +222,9 @@ def tile_cin_pb_v_kernel(tc, h2, x0, W3, b3, pre, grad_out, out):
             nc.sync.dma_start(out=out_rows[:, first : first + width, :], in_=result[:])
 
         z_head = keep.tile([P, HEAD, PASSES, F_H, PACK], BF16, align_bytes=64)
-        multiply_pass(z_head, 0, 0, HEAD_SHARE, h2_early[:].bitcast(BF16))
+        for_vector, for_gpsimd = slice(0, F_H - HEAD_SHARE), slice(F_H - HEAD_SHARE, F_H)
+        multiply_pass(nc.vector, z_head, slice(0, HEAD), 0, 0, for_vector, h2_early[:].bitcast(BF16))
+        multiply_pass(nc.gpsimd, z_head, slice(0, HEAD), 0, 0, for_gpsimd, h2_tok[:, 0])
         x0_late_turned = turn_x0(x0_late_rows)
         copy_x0(x0_late_turned, 1, slice(0, F_X), nc.vector.tensor_copy)
         turn_h2(0, h2_psum[:, 0])
@@ -233,7 +241,8 @@ def tile_cin_pb_v_kernel(tc, h2, x0, W3, b3, pre, grad_out, out):
             mask = keep.tile([P, N, PACK], BF16, name="mask%d" % c)
             nc.scalar.activation(out=mask[:], in_=sign[:], func=ACT.Relu)
             mask_of.append(mask)
-        multiply_pass(z_head, 0, 1, HEAD_SHARE, h2_psum[:, 1].bitcast(BF16))
+        multiply_pass(nc.vector, z_head, slice(0, HEAD), 0, 1, for_vector, h2_psum[:, 1].bitcast(BF16))
+        multiply_pass(nc.gpsimd, z_head, slice(0, HEAD), 0, 1, for_gpsimd, h2_tok[:, 1])
         copy_x0(x0_late_turned, 0, slice(X_EARLY, F_X), nc.scalar.copy)
         for c in range(PASSES):
             for first in range(0, N, N_BANK):
@@ -254,6 +263,22 @@ def tile_cin_pb_v_kernel(tc, h2, x0, W3, b3, pre, grad_out, out):
                     in1=grad_tok[:],
                     op=ALU.mult,
                 )
+        allocate(0)
+        first, width, share = pieces[0]
+        x0_diag = keep.tile([P, DIAG, PASSES, PACK], F32)
+        nc.scalar.copy(out=x0_diag[:], in_=x0_tok[:, first + width - DIAG : first + width])
+        for i in range(DIAG):
+            z_bank = psum.tile([P, PASSES, PACK, F_H], BF16, tag="bank")
+            for c in range(PASSES):
+                diagonal = diagonals.tile([P, PACK, P], BF16)
+                for j in range(PACK):
+                    nc.scalar.activation(
+                        out=diagonal[:, j, :], in_=identity[:], func=ACT.Copy, scale=x0_diag[:, i, c, j : j + 1]
+                    )
+                    nc.tensor.matmul(
+                        out=z_bank[:, c, j, :], lhsT=diagonal[:, j, :], rhs=h2_tok[:, c, :, j], start=True, stop=True
+                    )
+            nc.scalar.copy(out=z_tiles[0][:, width - DIAG + i], in_=z_bank[:].rearrange("p c j f -> p c f j"))
         nc.vector.quantize_mx(
             out=dp_codes[:].rearrange("p c n -> p (c n)").bitcast(E5M2X4),
             scales=dp_scales[:].rearrange("p c n -> p (c n)"),
@@ -263,14 +288,15 @@ def tile_cin_pb_v_kernel(tc, h2, x0, W3, b3, pre, grad_out, out):
         for start in range(0, HEAD, WIDEST):
             if start == HEAD - 2 * WIDEST:
                 product(0)
-            store(start, finish(z_head, start, WIDEST), nc.scalar.copy)
+            store(start, multiply(*quantise(z_head, start, WIDEST)), nc.scalar.copy)
         left = []
         for index, (first, width, share) in enumerate(pieces):
             if index < len(pieces) - 1:
                 product(index + 1)
-            sums = finish(z_tiles[index], 0, width)
+            sums = multiply(*quantise(z_tiles[index], 0, width))
             if index < len(pieces) - LAST:
-                store(first, sums, nc.scalar.copy)
+                for start in range(0, width, STORED):
+                    store(first + start, sums[start : start + STORED], nc.scalar.copy)
             else:
                 left.append((first, sums))
         for first, sums in left:

@@ -22,6 +22,7 @@ TILES = F_X
 WIDEST = 4
 HEAD = 24
 HEAD_SHARE = 20
+F_FIRST = 64
 X_EARLY = 32
 STEADY = 8
 SHARE = 16
@@ -59,6 +60,10 @@ def tile_cin_pb_v_kernel(tc, h2, x0, W3, b3, pre, grad_out, out):
         fixed = ctx.enter_context(tc.psum_pool(name="fixed", bufs=1))
         ctx.enter_context(tc.manual_schedule())
 
+        warm = keep.tile([P, 2], F32)
+        nc.vector.memset(warm[:], 0.0)
+        nc.scalar.activation(out=warm[:, 1:2], in_=warm[:, 0:1], func=ACT.Sign)
+
         x0_early_rows = keep.tile([P, TOKENS], BF16)
         x0_late_rows = keep.tile([P, TOKENS], BF16)
 
@@ -71,20 +76,21 @@ def tile_cin_pb_v_kernel(tc, h2, x0, W3, b3, pre, grad_out, out):
         load_x0(x0_early_rows, 0, slice(0, X_EARLY))
         nc.vector.memset(x0_early_rows[X_EARLY : 2 * X_EARLY, :], 0.0)
         nc.vector.memset(x0_early_rows[2 * X_EARLY : P, :], 0.0)
-        nc.vector.memset(x0_late_rows[0:X_EARLY, :], 0.0)
+        h2_first_rows = keep.tile([P, TOKENS], BF16)
+        nc.vector.memset(h2_first_rows[F_FIRST:F_H, :], 0.0)
         h2_rows = []
         for c in range(PASSES):
             rows = keep.tile([P, TOKENS], BF16, name="h2_rows%d" % c)
             h2_rows.append(rows)
 
-        def load_h2(queue, c, fields):
-            queue.dma_start(
-                out=h2_rows[c][fields, :].rearrange("f (b d) -> f b d", d=D),
+        def load_h2(rows, c, fields):
+            nc.sync.dma_start(
+                out=rows[fields, :].rearrange("f (b d) -> f b d", d=D),
                 in_=h2[c * B_PASS : (c + 1) * B_PASS, fields, :].rearrange("b f d -> f b d"),
             )
 
-        load_h2(nc.scalar, 0, slice(0, F_H // 2))
-        load_h2(nc.sync, 0, slice(F_H // 2, F_H))
+        load_h2(h2_first_rows, 0, slice(0, F_FIRST))
+        load_h2(h2_rows[0], 0, slice(F_FIRST, F_H))
         pre_rows = pre.rearrange("b d n -> (b d) n").rearrange("(c p j) n -> c p j n", c=PASSES, j=PACK)
         pre_sb = []
 
@@ -96,19 +102,16 @@ def tile_cin_pb_v_kernel(tc, h2, x0, W3, b3, pre, grad_out, out):
         load_pre(0)
         load_x0(x0_late_rows, 0, slice(X_EARLY, F_X))
         load_x0(x0_late_rows, 1, slice(0, F_X))
-        load_h2(nc.sync, 1, slice(0, F_H))
+        load_h2(h2_rows[1], 1, slice(0, F_H))
         grad_rows = keep.tile([P, N], BF16)
         nc.sync.dma_start(out=grad_rows[0:B, :], in_=grad_out)
-        nc.vector.memset(grad_rows[B : 2 * B, :], 0.0)
-        nc.vector.memset(grad_rows[2 * B : P, :], 0.0)
         load_pre(1)
-
-        warm = keep.tile([P, 2], F32)
-        nc.vector.memset(warm[:], 0.0)
-        nc.scalar.activation(out=warm[:, 1:2], in_=warm[:, 0:1], func=ACT.Sign)
 
         identity = keep.tile([P, P], F32)
         make_identity(nc, identity[:])
+        nc.gpsimd.memset(x0_late_rows[0:X_EARLY, :], 0.0)
+        nc.gpsimd.memset(grad_rows[B : 2 * B, :], 0.0)
+        nc.gpsimd.memset(grad_rows[2 * B : P, :], 0.0)
         spread = keep.tile([P, B, P // B_PASS], BF16)
         nc.vector.tensor_copy(
             out=spread[:], in_=identity[:, 0:B].unsqueeze(2).to_broadcast([P, B, P // B_PASS])
@@ -133,19 +136,23 @@ def tile_cin_pb_v_kernel(tc, h2, x0, W3, b3, pre, grad_out, out):
 
         copy_x0(turn_x0(x0_early_rows), 0, slice(0, X_EARLY), nc.vector.tensor_copy)
 
-        def turn_h2(c, turned):
-            words = h2_rows[c][:].bitcast(F32).rearrange("f (p u) -> f u p", u=2)
+        def turn_h2(rows, turned):
+            words = rows[:].bitcast(F32).rearrange("f (p u) -> f u p", u=2)
             for u in range(2):
                 nc.tensor.transpose(out=turned[:, :, u], in_=words[:, u, :], identity=identity[:])
 
-        h2_early = psum.tile([P, F_H, 2], F32, tag="bank")
-        turn_h2(0, h2_early)
+        nc.scalar.copy(out=h2_rows[0][0:F_FIRST].bitcast(F32), in_=h2_first_rows[0:F_FIRST].bitcast(F32))
+        h2_early = []
+        for rows in (h2_first_rows, h2_rows[0]):
+            turned = psum.tile([P, F_H, 2], F32, tag="bank")
+            turn_h2(rows, turned)
+            h2_early.append(turned)
         h2_psum = fixed.tile([P, PASSES, F_H, 2], F32)
         h2_tok = keep.tile([P, PASSES, F_H, PACK], BF16)
 
         def copy_h2(c, copy):
             turned = psum.tile([P, F_H, 2], F32, tag="bank")
-            turn_h2(c, turned)
+            turn_h2(h2_rows[c], turned)
             copy(out=h2_tok[:, c].bitcast(F32), in_=turned[:])
 
         copy_h2(0, nc.scalar.copy)
@@ -223,13 +230,14 @@ def tile_cin_pb_v_kernel(tc, h2, x0, W3, b3, pre, grad_out, out):
 
         z_head = keep.tile([P, HEAD, PASSES, F_H, PACK], BF16, align_bytes=64)
         for_vector, for_gpsimd = slice(0, F_H - HEAD_SHARE), slice(F_H - HEAD_SHARE, F_H)
-        multiply_pass(nc.vector, z_head, slice(0, HEAD), 0, 0, for_vector, h2_early[:].bitcast(BF16))
+        for turned, fields in zip(h2_early, (slice(0, F_FIRST), slice(F_FIRST, F_H - HEAD_SHARE))):
+            multiply_pass(nc.vector, z_head, slice(0, HEAD), 0, 0, fields, turned[:].bitcast(BF16))
         multiply_pass(nc.gpsimd, z_head, slice(0, HEAD), 0, 0, for_gpsimd, h2_tok[:, 0])
         x0_late_turned = turn_x0(x0_late_rows)
         copy_x0(x0_late_turned, 1, slice(0, F_X), nc.vector.tensor_copy)
-        turn_h2(0, h2_psum[:, 0])
+        turn_h2(h2_rows[0], h2_psum[:, 0])
         copy_h2(1, nc.vector.tensor_copy)
-        turn_h2(1, h2_psum[:, 1])
+        turn_h2(h2_rows[1], h2_psum[:, 1])
 
         dp_codes = keep.tile([P, PASSES, N], U32, align_bytes=64)
         dp_scales = keep.tile([P, PASSES, N], U8, align_bytes=64)
@@ -295,8 +303,9 @@ def tile_cin_pb_v_kernel(tc, h2, x0, W3, b3, pre, grad_out, out):
                 product(index + 1)
             sums = multiply(*quantise(z_tiles[index], 0, width))
             if index < len(pieces) - LAST:
-                for start in range(0, width, STORED):
-                    store(first + start, sums[start : start + STORED], nc.scalar.copy)
+                stored = STORED if width == WIDEST else 1
+                for start in range(0, width, stored):
+                    store(first + start, sums[start : start + stored], nc.scalar.copy)
             else:
                 left.append((first, sums))
         for first, sums in left:

@@ -93,10 +93,13 @@ def tile_cin_pb_v_kernel(tc, h2, x0, W3, b3, pre, grad_out, out):
         load_h2(h2_rows[0], 0, slice(F_FIRST, F_H))
         pre_rows = pre.rearrange("b d n -> (b d) n").rearrange("(c p j) n -> c p j n", c=PASSES, j=PACK)
         pre_sb = []
+        halves = (slice(0, N // 2), slice(N // 2, N))
+        pre_columns = (halves, (slice(0, N),))
 
         def load_pre(c):
             pre_c = keep.tile([P, PACK, N], F32, name="pre_sb%d" % c)
-            nc.sync.dma_start(out=pre_c[:], in_=pre_rows[c])
+            for cols in pre_columns[c]:
+                nc.sync.dma_start(out=pre_c[:, :, cols], in_=pre_rows[c][:, :, cols])
             pre_sb.append(pre_c)
 
         load_pre(0)
@@ -245,7 +248,12 @@ def tile_cin_pb_v_kernel(tc, h2, x0, W3, b3, pre, grad_out, out):
         mask_of = []
         for c in range(PASSES):
             sign = keep.tile([P, N, PACK], BF16, name="sign%d" % c)
-            nc.scalar.activation(out=sign[:], in_=pre_sb[c][:].rearrange("p j n -> p n j"), func=ACT.Sign)
+            for cols in pre_columns[c]:
+                nc.scalar.activation(
+                    out=sign[:, cols].rearrange("p (m i) j -> p m j i", i=4),
+                    in_=pre_sb[c][:, :, cols].rearrange("p j (m i) -> p m j i", i=4),
+                    func=ACT.Sign,
+                )
             mask = keep.tile([P, N, PACK], BF16, name="mask%d" % c)
             nc.scalar.activation(out=mask[:], in_=sign[:], func=ACT.Relu)
             mask_of.append(mask)

from contextlib import ExitStack

import concourse.mybir as mybir
from concourse.masks import make_identity

F32 = mybir.dt.float32
BF16 = mybir.dt.bfloat16
U32 = mybir.dt.uint32
U8 = mybir.dt.uint8
E4M3X4 = mybir.dt.float8_e4m3fn_x4
E5M2X4 = mybir.dt.float8_e5m2_x4
ALU = mybir.AluOpType
ACT = mybir.ActivationFunctionType

P = 128
PACK = 4
PASSES = 2
B, F_H, F_X, D, N = 32, 128, 64, 32, 512
B_PASS = B // PASSES
TOKENS = B_PASS * D
TILES = F_X
WIDEST = 4
HEAD = 24
HEAD_SHARE = 20
F_FIRST = 64
X_EARLY = 32
STEADY = 8
SHARE = 16
BUFFERS = 3
STORED = 2
N_BANK = 256
N_PLAIN = 128
DIAG = 1
LAST = 3

FLOPS = 2 * B * D * F_H * F_X * N
BYTES = 2 * (B * F_H * D + B * F_X * D + B * N) + 4 * B * D * N + 4 * F_H * F_X * N


def cut_into_pieces():
    widths = [WIDEST] * STEADY + [2, 2, 1, 1, 1, 1]
    pieces = []
    first = HEAD
    for index, width in enumerate(widths):
        pieces.append((first, width, SHARE if width > 1 and not 0 < index < BUFFERS else 0))
        first += width
    assert first == TILES
    return pieces


def tile_cin_pb_v_kernel(tc, h2, x0, W3, b3, pre, grad_out, out):
    nc = tc.nc
    with ExitStack() as ctx:
        keep = ctx.enter_context(tc.tile_pool(name="keep", bufs=1))
        products = ctx.enter_context(tc.tile_pool(name="products", bufs=BUFFERS))
        quantised = ctx.enter_context(tc.tile_pool(name="quantised", bufs=8))
        diagonals = ctx.enter_context(tc.tile_pool(name="diagonals", bufs=2))
        results = ctx.enter_context(tc.tile_pool(name="results", bufs=8))
        psum = ctx.enter_context(tc.psum_pool(name="psum", bufs=7))
        fixed = ctx.enter_context(tc.psum_pool(name="fixed", bufs=1))
        ctx.enter_context(tc.manual_schedule())

        warm = keep.tile([P, 2], F32)
        nc.vector.memset(warm[:], 0.0)
        nc.scalar.activation(out=warm[:, 1:2], in_=warm[:, 0:1], func=ACT.Sign)

        x0_early_rows = keep.tile([P, TOKENS], BF16)
        x0_late_rows = keep.tile([P, TOKENS], BF16)

        def load_x0(rows, c, fields):
            nc.sync.dma_start(
                out=rows[c * F_X + fields.start : c * F_X + fields.stop, :].rearrange("g (b d) -> g b d", d=D),
                in_=x0[c * B_PASS : (c + 1) * B_PASS, fields].rearrange("b g d -> g b d"),
            )

        load_x0(x0_early_rows, 0, slice(0, X_EARLY))
        nc.vector.memset(x0_early_rows[X_EARLY : 2 * X_EARLY, :], 0.0)
        nc.vector.memset(x0_early_rows[2 * X_EARLY : P, :], 0.0)
        h2_first_rows = keep.tile([P, TOKENS], BF16)
        nc.vector.memset(h2_first_rows[F_FIRST:F_H, :], 0.0)
        h2_rows = []
        for c in range(PASSES):
            rows = keep.tile([P, TOKENS], BF16, name="h2_rows%d" % c)
            h2_rows.append(rows)

        def load_h2(rows, c, fields):
            nc.sync.dma_start(
                out=rows[fields, :].rearrange("f (b d) -> f b d", d=D),
                in_=h2[c * B_PASS : (c + 1) * B_PASS, fields, :].rearrange("b f d -> f b d"),
            )

        load_h2(h2_first_rows, 0, slice(0, F_FIRST))
        load_h2(h2_rows[0], 0, slice(F_FIRST, F_H))
        pre_rows = pre.rearrange("b d n -> (b d) n").rearrange("(c p j) n -> c p j n", c=PASSES, j=PACK)
        pre_sb = []
        halves = (slice(0, N // 2), slice(N // 2, N))
        pre_columns = (halves, (slice(0, N),))

        def load_pre(c):
            pre_c = keep.tile([P, PACK, N], F32, name="pre_sb%d" % c)
            for cols in pre_columns[c]:
                nc.sync.dma_start(out=pre_c[:, :, cols], in_=pre_rows[c][:, :, cols])
            pre_sb.append(pre_c)

        load_pre(0)
        load_x0(x0_late_rows, 0, slice(X_EARLY, F_X))
        load_x0(x0_late_rows, 1, slice(0, F_X))
        load_h2(h2_rows[1], 1, slice(0, F_H))
        grad_rows = keep.tile([P, N], BF16)
        nc.sync.dma_start(out=grad_rows[0:B, :], in_=grad_out)
        load_pre(1)

        identity = keep.tile([P, P], F32)
        make_identity(nc, identity[:])
        nc.gpsimd.memset(x0_late_rows[0:X_EARLY, :], 0.0)
        nc.gpsimd.memset(grad_rows[B : 2 * B, :], 0.0)
        nc.gpsimd.memset(grad_rows[2 * B : P, :], 0.0)
        spread = keep.tile([P, B, P // B_PASS], BF16)
        nc.vector.tensor_copy(
            out=spread[:], in_=identity[:, 0:B].unsqueeze(2).to_broadcast([P, B, P // B_PASS])
        )
        spread_cols = spread[:].rearrange("k b r -> k (b r)")

        def turn_x0(rows):
            words = rows[:].bitcast(F32).rearrange("q (p u) -> q u p", u=2)
            turned = psum.tile([P, 2, PASSES, F_X], F32, tag="bank")
            for u in range(2):
                nc.tensor.transpose(
                    out=turned[:, u].rearrange("p c g -> p (c g)"), in_=words[:, u, :], identity=identity[:]
                )
            return turned

        x0_tok = keep.tile([P, F_X, PASSES, PACK], BF16)

        def copy_x0(turned, c, fields, copy):
            copy(
                out=x0_tok[:].bitcast(F32)[:, fields, c], in_=turned[:, :, c, fields].rearrange("p u g -> p g u")
            )

        copy_x0(turn_x0(x0_early_rows), 0, slice(0, X_EARLY), nc.vector.tensor_copy)

        def turn_h2(rows, turned):
            words = rows[:].bitcast(F32).rearrange("f (p u) -> f u p", u=2)
            for u in range(2):
                nc.tensor.transpose(out=turned[:, :, u], in_=words[:, u, :], identity=identity[:])

        nc.scalar.copy(out=h2_rows[0][0:F_FIRST].bitcast(F32), in_=h2_first_rows[0:F_FIRST].bitcast(F32))
        h2_early = []
        for rows in (h2_first_rows, h2_rows[0]):
            turned = psum.tile([P, F_H, 2], F32, tag="bank")
            turn_h2(rows, turned)
            h2_early.append(turned)
        h2_psum = fixed.tile([P, PASSES, F_H, 2], F32)
        h2_tok = keep.tile([P, PASSES, F_H, PACK], BF16)

        def copy_h2(c, copy):
            turned = psum.tile([P, F_H, 2], F32, tag="bank")
            turn_h2(h2_rows[c], turned)
            copy(out=h2_tok[:, c].bitcast(F32), in_=turned[:])

        copy_h2(0, nc.scalar.copy)

        pieces = cut_into_pieces()
        z_tiles = {}
        out_rows = out.rearrange("(f g) n -> f g n", g=F_X)

        def multiply_pass(engine, z, tiles, first, c, fields, h2_c):
            shape = [P, tiles.stop - tiles.start, fields.stop - fields.start, PACK]
            engine.tensor_tensor(
                out=z[:, tiles, c, fields],
                in0=x0_tok[:, first + tiles.start : first + tiles.stop, c].unsqueeze(2).to_broadcast(shape),
                in1=h2_c[:, fields].unsqueeze(1).to_broadcast(shape),
                op=ALU.mult,
            )

        def allocate(index):
            first, width, share = pieces[index]
            z = products.tile([P, width, PASSES, F_H, PACK], BF16, name="z", align_bytes=64)
            z_tiles[index] = z

        def product(index):
            if index > 0:
                allocate(index)
            first, width, share = pieces[index]
            own = width - DIAG if index == 0 else width
            x0_both = x0_tok[:, first : first + own].unsqueeze(3)
            for engine, fields, h2_both in (
                (nc.vector, slice(0, F_H - share), h2_psum[:].bitcast(BF16)),
                (nc.gpsimd, slice(F_H - share, F_H), h2_tok[:]),
            ):
                shape = [P, own, PASSES, fields.stop - fields.start, PACK]
                if fields.start < fields.stop:
                    engine.tensor_tensor(
                        out=z_tiles[index][:, 0:own, :, fields],
                        in0=x0_both.to_broadcast(shape),
                        in1=h2_both[:, :, fields].unsqueeze(1).to_broadcast(shape),
                        op=ALU.mult,
                    )

        def quantise(z, start, width):
            z_codes = quantised.tile([P, width, PASSES, P], U32, align_bytes=64)
            z_scales = quantised.tile([P, width, PASSES, P], U8, align_bytes=64)
            nc.vector.quantize_mx(
                out=z_codes[:].rearrange("p i c m -> p (i c m)").bitcast(E4M3X4),
                scales=z_scales[:].rearrange("p i c m -> p (i c m)"),
                in_=z[:, start : start + width].rearrange("p i c f j -> p (i c f j)"),
            )
            return z_codes, z_scales

        def multiply(z_codes, z_scales):
            sums = []
            for i in range(z_codes.shape[1]):
                acc = psum.tile([P, N], F32, tag="bank")
                sums.append(acc)
                for c in range(PASSES):
                    nc.tensor.matmul_mx(
                        out=acc[:],
                        lhsT=z_codes[:, i, c, :].bitcast(E4M3X4),
                        lhsT_scale=z_scales[:, i, c, :],
                        rhs=dp_codes[:, c, :].bitcast(E5M2X4),
                        rhs_scale=dp_scales[:, c, :],
                        start=(c == 0),
                        stop=(c == PASSES - 1),
                    )
            return sums

        def store(first, sums, copy):
            width = len(sums)
            result = results.tile([P, width, N], F32)
            for i in range(width):
                copy(out=result[:, i, :], in_=sums[i][:])
            nc.sync.dma_start(out=out_rows[:, first : first + width, :], in_=result[:])

        z_head = keep.tile([P, HEAD, PASSES, F_H, PACK], BF16, align_bytes=64)
        for_vector, for_gpsimd = slice(0, F_H - HEAD_SHARE), slice(F_H - HEAD_SHARE, F_H)
        for turned, fields in zip(h2_early, (slice(0, F_FIRST), slice(F_FIRST, F_H - HEAD_SHARE))):
            multiply_pass(nc.vector, z_head, slice(0, HEAD), 0, 0, fields, turned[:].bitcast(BF16))
        multiply_pass(nc.gpsimd, z_head, slice(0, HEAD), 0, 0, for_gpsimd, h2_tok[:, 0])
        x0_late_turned = turn_x0(x0_late_rows)
        copy_x0(x0_late_turned, 1, slice(0, F_X), nc.vector.tensor_copy)
        turn_h2(h2_rows[0], h2_psum[:, 0])
        copy_h2(1, nc.vector.tensor_copy)
        turn_h2(h2_rows[1], h2_psum[:, 1])

        dp_codes = keep.tile([P, PASSES, N], U32, align_bytes=64)
        dp_scales = keep.tile([P, PASSES, N], U8, align_bytes=64)
        dp = keep.tile([P, PASSES, N, PACK], BF16, align_bytes=64)
        mask_of = []
        for c in range(PASSES):
            sign = keep.tile([P, N, PACK], BF16, name="sign%d" % c)
            for cols in pre_columns[c]:
                nc.scalar.activation(
                    out=sign[:, cols].rearrange("p (m i) j -> p m j i", i=4),
                    in_=pre_sb[c][:, :, cols].rearrange("p j (m i) -> p m j i", i=4),
                    func=ACT.Sign,
                )
            mask = keep.tile([P, N, PACK], BF16, name="mask%d" % c)
            nc.scalar.activation(out=mask[:], in_=sign[:], func=ACT.Relu)
            mask_of.append(mask)
        multiply_pass(nc.vector, z_head, slice(0, HEAD), 0, 1, for_vector, h2_psum[:, 1].bitcast(BF16))
        multiply_pass(nc.gpsimd, z_head, slice(0, HEAD), 0, 1, for_gpsimd, h2_tok[:, 1])
        copy_x0(x0_late_turned, 0, slice(X_EARLY, F_X), nc.scalar.copy)
        for c in range(PASSES):
            for first in range(0, N, N_BANK):
                grad_tok = psum.tile([P, N_BANK, PACK], BF16, tag="bank")
                for inside in range(0, N_BANK, N_PLAIN):
                    nc.tensor.matmul(
                        out=grad_tok[:, inside : inside + N_PLAIN, :].rearrange("p n j -> p (n j)"),
                        lhsT=spread_cols[:, c * P : (c + 1) * P],
                        rhs=grad_rows[:, first + inside : first + inside + N_PLAIN]
                        .unsqueeze(2)
                        .to_broadcast([P, N_PLAIN, PACK]),
                        start=True,
                        stop=True,
                    )
                nc.vector.tensor_tensor(
                    out=dp[:, c, first : first + N_BANK, :],
                    in0=mask_of[c][:, first : first + N_BANK, :],
                    in1=grad_tok[:],
                    op=ALU.mult,
                )
        allocate(0)
        first, width, share = pieces[0]
        x0_diag = keep.tile([P, DIAG, PASSES, PACK], F32)
        nc.scalar.copy(out=x0_diag[:], in_=x0_tok[:, first + width - DIAG : first + width])
        for i in range(DIAG):
            z_bank = psum.tile([P, PASSES, PACK, F_H], BF16, tag="bank")
            for c in range(PASSES):
                diagonal = diagonals.tile([P, PACK, P], BF16)
                for j in range(PACK):
                    nc.scalar.activation(
                        out=diagonal[:, j, :], in_=identity[:], func=ACT.Copy, scale=x0_diag[:, i, c, j : j + 1]
                    )
                    nc.tensor.matmul(
                        out=z_bank[:, c, j, :], lhsT=diagonal[:, j, :], rhs=h2_tok[:, c, :, j], start=True, stop=True
                    )
            nc.scalar.copy(out=z_tiles[0][:, width - DIAG + i], in_=z_bank[:].rearrange("p c j f -> p c f j"))
        nc.vector.quantize_mx(
            out=dp_codes[:].rearrange("p c n -> p (c n)").bitcast(E5M2X4),
            scales=dp_scales[:].rearrange("p c n -> p (c n)"),
            in_=dp[:].rearrange("p c n j -> p (c n j)"),
        )

        for start in range(0, HEAD, WIDEST):
            if start == HEAD - 2 * WIDEST:
                product(0)
            store(start, multiply(*quantise(z_head, start, WIDEST)), nc.scalar.copy)
        left = []
        for index, (first, width, share) in enumerate(pieces):
            if index < len(pieces) - 1:
                product(index + 1)
            sums = multiply(*quantise(z_tiles[index], 0, width))
            if index < len(pieces) - LAST:
                stored = STORED if width == WIDEST else 1
                for start in range(0, width, stored):
                    store(first + start, sums[start : start + stored], nc.scalar.copy)
            else:
                left.append((first, sums))
        for first, sums in left:
            store(first, sums, nc.vector.tensor_copy)
